import numpy as np
import ml_dtypes


def mxq(x, axis, fmt="e4m3"):
    dtype, down = {"e4m3": (ml_dtypes.float8_e4m3fn, 7), "e5m2": (ml_dtypes.float8_e5m2, 14)}[fmt]
    v = np.moveaxis(np.asarray(x, np.float32).astype(ml_dtypes.bfloat16).astype(np.float64), axis, -1)
    blocks = v.reshape(v.shape[:-1] + (-1, 32))
    amax = np.abs(blocks).max(-1, keepdims=True)
    byte = np.maximum(np.where(amax > 0, np.frexp(amax)[1] - 1 + 127, 0) - down, 1)
    scale = np.exp2(byte - 127.0)
    codes = (blocks / scale).astype(np.float32).astype(dtype).astype(np.float64)
    return np.moveaxis((codes * scale).reshape(v.shape), -1, axis)


WIDE = False


def mx_kscale(k):
    if not WIDE:
        return np.ones(k)
    levels = np.array([10, -10, 5, -5, 0])
    a = np.random.permutation(np.resize(levels, k // 512 * 4)).reshape(k // 512, 4)
    idx = np.arange(k)
    return np.exp2(a[idx // 512, idx % 128 // 32])


BF16 = ml_dtypes.bfloat16


def bf(x):
    return np.asarray(x, np.float32).astype(BF16)


def f64(x):
    return np.asarray(x).astype(np.float64)


E2M1 = np.array([0.0, 0.5, 1.0, 1.5, 2.0, 3.0, 4.0, 6.0, -0.0, -0.5, -1.0, -1.5, -2.0, -3.0, -4.0, -6.0])


def pack_weight(w, fmt):
    k, n = w.shape
    w = f64(bf(w)).reshape(k // 32, 32, n)
    amax = np.abs(w).max(1)
    if fmt == "e4m3":
        byte = np.frexp(amax)[1] - 1 + 127 - 7
    else:
        mant, ex = np.frexp(amax / 6.0)
        byte = np.where(mant > 0.5, ex, ex - 1) + 127
    byte = np.clip(np.where(amax > 0, byte, 1), 1, 254)
    scaled = (w * np.exp2(127.0 - byte)[:, None, :]).reshape(k, n).astype(np.float32)
    by_word = np.ascontiguousarray(scaled.reshape(k // 512, 128, 4, n).transpose(0, 1, 3, 2))
    if fmt == "e4m3":
        words = by_word.astype(ml_dtypes.float8_e4m3fn).view(np.uint8)
    else:
        c = by_word.astype(ml_dtypes.float4_e2m1fn).view(np.uint8) & 0xF
        words = c[..., 0::2] | (c[..., 1::2] << 4)
    return np.ascontiguousarray(words), np.ascontiguousarray(byte.astype(np.uint8).reshape(k // 512, 16, n))


def unpack_weight(words, scales, fmt):
    g, p, n, _ = words.shape
    if fmt == "e4m3":
        vals = np.ascontiguousarray(words).view(ml_dtypes.float8_e4m3fn).astype(np.float64)
    else:
        nib = np.empty((g, p, n, 4), np.uint8)
        nib[..., 0::2] = words & 0xF
        nib[..., 1::2] = words >> 4
        vals = E2M1[nib]
    vals = vals * np.repeat(np.exp2(scales.astype(np.float64) - 127.0), 8, axis=1)[..., None]
    return vals.transpose(0, 1, 3, 2).reshape(g * 512, n)

def pack4(w):
    words, scales = pack_weight(w, "e2m1")
    return words.reshape(words.shape[0], 128, -1), scales


def unpack4(words, scales):
    return unpack_weight(words.reshape(words.shape[0], 128, -1, 2), scales, "e2m1")


B, D = 2048, 1024


def softplus(v):
    return np.logaddexp(v, 0.0)


def setup_inputs():
    s = mx_kscale(D)
    xt = bf(np.random.standard_normal((B, D)) * 1.3 * s)
    eps = bf(np.random.standard_normal((B, D)))
    x = bf(np.random.standard_normal((B, D)))
    t_rand = bf(np.random.uniform(0.0, 1.0, (B, 1)))
    Wm_words, Wm_scales = pack4((np.random.standard_normal((D, D)) / np.sqrt(D) / s[None, :]).T)
    bm = bf(np.random.standard_normal(D) * 0.5)
    Wv_words, Wv_scales = pack4((np.random.standard_normal((D, D)) / np.sqrt(D) / s[None, :]).T)
    bv = bf(np.random.standard_normal(D) * 0.5)
    return {"xt": xt, "eps": eps, "x": x, "t_rand": t_rand,
            "Wm_words": Wm_words, "Wm_scales": Wm_scales, "bm": bm,
            "Wv_words": Wv_words, "Wv_scales": Wv_scales, "bv": bv}


def reference(xt, eps, x, t_rand, Wm_words, Wm_scales, bm, Wv_words, Wv_scales, bv):
    xq = mxq(f64(xt), 1, "e4m3")
    mu = (xq @ unpack4(Wm_words, Wm_scales)) + f64(bm)
    sigma = softplus((xq @ unpack4(Wv_words, Wv_scales)) + f64(bv))
    x_prime = mu + sigma * f64(eps)
    return (1.0 - f64(t_rand)) * f64(x) + f64(t_rand) * x_prime

@@ -1,0 +1,226 @@
+from contextlib import ExitStack
+
+import concourse.mybir as mybir
+from concourse.masks import make_identity
+
+F32 = mybir.dt.float32
+BF16 = mybir.dt.bfloat16
+I32 = mybir.dt.int32
+U32 = mybir.dt.uint32
+U8 = mybir.dt.uint8
+FP8X4 = mybir.dt.float8_e4m3fn_x4
+FP4X4 = mybir.dt.float4_e2m1fn_x4
+ALU = mybir.AluOpType
+ACT = mybir.ActivationFunctionType
+
+P = 128
+ROWS = 2048
+FEATURES = 1024
+PACK = 4
+K_PASS = P * PACK
+PASSES = FEATURES // K_PASS
+ROW_TILES = ROWS // P
+BATCH = 4
+BATCHES = ROW_TILES // BATCH
+BANK = 512
+HALVES = FEATURES // BANK
+WORDS = K_PASS // 2
+SPREAD, MEAN = 0, 1
+LN_FLOOR = 2.0**-60
+
+FLOPS = 2 * ROWS * FEATURES * 2 * FEATURES
+
+
+def tile_diffscm_pb_kernel(
+    tc, xt, eps, x, t_rand, Wm_words, Wm_scales, bm, Wv_words, Wv_scales, bv, out
+):
+    nc = tc.nc
+    xt_rows = xt.rearrange("(p i) d -> p i d", i=ROW_TILES)
+    eps_rows = eps.rearrange("(p i) d -> p i d", i=ROW_TILES)
+    x_rows = x.rearrange("(p i) d -> p i d", i=ROW_TILES)
+    out_rows = out.rearrange("(p i) d -> p i d", i=ROW_TILES)
+
+    with ExitStack() as ctx:
+        const = ctx.enter_context(tc.tile_pool(name="const", bufs=1))
+        loads = ctx.enter_context(tc.tile_pool(name="loads", bufs=2))
+        regroup = ctx.enter_context(tc.tile_pool(name="regroup", bufs=1))
+        packed = ctx.enter_context(tc.tile_pool(name="packed", bufs=2))
+        work = ctx.enter_context(tc.tile_pool(name="work", bufs=2))
+        flip_banks = ctx.enter_context(tc.psum_pool(name="flip_banks", bufs=2))
+        sum_banks = ctx.enter_context(tc.psum_pool(name="sum_banks", bufs=6))
+        ctx.enter_context(tc.manual_schedule())
+
+        def load_batch(source, k, label):
+            rows = loads.tile([P, BATCH, FEATURES], BF16, name=label, tag=label)
+            nc.sync.dma_start(out=rows[:], in_=source[:, k * BATCH : (k + 1) * BATCH, :])
+            return rows
+
+        w_scales = const.tile([P, 2, PASSES, FEATURES], U8, align_bytes=64)
+        nc.vector.memset(w_scales[:].rearrange("p h g n -> p (h g n)").bitcast(I32), 0)
+        identity = const.tile([P, P], F32)
+        make_identity(nc, identity[:])
+
+        xt_of = {0: load_batch(xt_rows, 0, "xt_sb")}
+
+        w_words = const.tile([P, 2, PASSES, 2 * FEATURES], U8, align_bytes=64)
+        for head, words, scales in ((SPREAD, Wv_words, Wv_scales), (MEAN, Wm_words, Wm_scales)):
+            for quadrant in range(4):
+                nc.sync.dma_start(
+                    out=w_scales[32 * quadrant : 32 * quadrant + 4, head].bitcast(I32),
+                    in_=scales.bitcast(I32)[:, 4 * quadrant : 4 * quadrant + 4, :].rearrange(
+                        "g r w -> r g w"
+                    ),
+                )
+            nc.sync.dma_start(
+                out=w_words[:, head].bitcast(I32),
+                in_=words.bitcast(I32).rearrange("g p w -> p g w"),
+            )
+
+        t_bf = const.tile([P, ROW_TILES], BF16)
+        nc.scalar.dma_start(out=t_bf[:], in_=t_rand.rearrange("(p i) o -> p (i o)", i=ROW_TILES))
+        bias_rows = const.tile([P, 2, FEATURES], BF16)
+        nc.scalar.dma_start(out=bias_rows[:, SPREAD, :], in_=bv.partition_broadcast(P))
+        nc.scalar.dma_start(out=bias_rows[:, MEAN, :], in_=bm.partition_broadcast(P))
+        t_new = const.tile([P, ROW_TILES], F32)
+        nc.vector.tensor_copy(out=t_new[:], in_=t_bf[:])
+        t_old = const.tile([P, ROW_TILES], F32)
+        nc.vector.tensor_scalar(
+            out=t_old[:], in0=t_bf[:], scalar1=-1.0, scalar2=1.0, op0=ALU.mult, op1=ALU.add
+        )
+
+        def transpose_batch(xt_sb):
+            grouped = regroup.tile([P, BATCH * PASSES * P * PACK], BF16, align_bytes=64)
+            grouped_words = grouped[:].bitcast(F32).rearrange(
+                "p (i g r u) -> p i g r u", i=BATCH, g=PASSES, u=2
+            )
+            for i in range(BATCH):
+                row_words = xt_sb[:, i, :].bitcast(F32)
+                flipped = flip_banks.tile([P, PASSES, 2, P], F32)
+                for g in range(PASSES):
+                    for u in range(2):
+                        nc.tensor.transpose(
+                            flipped[:, g, u, :],
+                            row_words[:, WORDS * g + u : WORDS * (g + 1) : 2],
+                            identity[:],
+                        )
+                nc.scalar.copy(
+                    out=grouped_words[:, i], in_=flipped[:].rearrange("p g u r -> p g r u")
+                )
+            return grouped
+
+        def quantise_batch(grouped):
+            codes = packed.tile([P, BATCH, PASSES, P], U32, align_bytes=64)
+            scales = packed.tile([P, BATCH, PASSES, P], U8, align_bytes=64)
+            nc.vector.quantize_mx(
+                out=codes[:].rearrange("p i g r -> p (i g r)").bitcast(FP8X4),
+                scales=scales[:].rearrange("p i g r -> p (i g r)"),
+                in_=grouped[:],
+            )
+            return codes, scales
+
+        def heads_of_batch(codes, scales):
+            pre = work.tile([P, 2, BATCH, FEATURES], F32)
+            gate = work.tile([P, BATCH, FEATURES], F32)
+            for i in range(BATCH):
+                for head in (SPREAD, MEAN):
+                    for half in range(HALVES):
+                        cols = slice(half * BANK, (half + 1) * BANK)
+                        sums = sum_banks.tile([P, BANK], F32)
+                        for g in range(PASSES):
+                            nc.tensor.matmul_mx(
+                                out=sums[:],
+                                lhsT=codes[:, i, g, :].bitcast(FP8X4),
+                                lhsT_scale=scales[:, i, g, :],
+                                rhs=w_words[
+                                    :, head, g, 2 * half * BANK : 2 * (half + 1) * BANK
+                                ].bitcast(FP4X4),
+                                rhs_scale=w_scales[:, head, g, cols],
+                                start=(g == 0),
+                                stop=(g == PASSES - 1),
+                            )
+                        nc.vector.tensor_tensor(
+                            out=pre[:, head, i, cols],
+                            in0=sums[:],
+                            in1=bias_rows[:, head, cols],
+                            op=ALU.add,
+                        )
+                nc.scalar.activation(
+                    out=gate[:, i, :], in_=pre[:, SPREAD, i, :], func=ACT.Sigmoid, scale=-1.0
+                )
+            return pre, gate
+
+        def log_of_batch(gate):
+            flat = gate[:].rearrange("p i n -> p (i n)")
+            nc.scalar.activation(out=flat, in_=flat, func=ACT.Ln, bias=LN_FLOOR)
+
+        def blend_batch(k, pre, gate, eps_sb, x_sb):
+            spread = pre[:, SPREAD].rearrange("p i n -> p (i n)")
+            nc.vector.scalar_tensor_tensor(
+                out=spread,
+                in0=gate[:].rearrange("p i n -> p (i n)"),
+                scalar=-1.0,
+                in1=spread,
+                op0=ALU.mult,
+                op1=ALU.max,
+            )
+            result = work.tile([P, BATCH, FEATURES], F32)
+            for step in range(BATCH + 2):
+                if step < BATCH:
+                    i = step
+                    nc.vector.scalar_tensor_tensor(
+                        out=pre[:, SPREAD, i, :],
+                        in0=pre[:, SPREAD, i, :],
+                        scalar=t_new[:, k * BATCH + i : k * BATCH + i + 1],
+                        in1=eps_sb[:, i, :],
+                        op0=ALU.mult,
+                        op1=ALU.mult,
+                    )
+                if 0 <= step - 1 < BATCH:
+                    i = step - 1
+                    nc.vector.scalar_tensor_tensor(
+                        out=pre[:, MEAN, i, :],
+                        in0=pre[:, MEAN, i, :],
+                        scalar=t_new[:, k * BATCH + i : k * BATCH + i + 1],
+                        in1=pre[:, SPREAD, i, :],
+                        op0=ALU.mult,
+                        op1=ALU.add,
+                    )
+                if 0 <= step - 2:
+                    i = step - 2
+                    nc.vector.scalar_tensor_tensor(
+                        out=result[:, i, :],
+                        in0=x_sb[:, i, :],
+                        scalar=t_old[:, k * BATCH + i : k * BATCH + i + 1],
+                        in1=pre[:, MEAN, i, :],
+                        op0=ALU.mult,
+                        op1=ALU.add,
+                    )
+                    nc.sync.dma_start(out=out_rows[:, k * BATCH + i, :], in_=result[:, i, :])
+
+        xt_of[1] = load_batch(xt_rows, 1, "xt_sb")
+        grouped_of = {0: transpose_batch(xt_of[0])}
+        packed_of = {0: quantise_batch(grouped_of[0])}
+        xt_of[2] = load_batch(xt_rows, 2, "xt_sb")
+        grouped_of[1] = transpose_batch(xt_of[1])
+        xt_of[3] = load_batch(xt_rows, 3, "xt_sb")
+        eps_of = {}
+        x_of = {}
+        for k in range(2):
+            eps_of[k] = load_batch(eps_rows, k, "eps_sb")
+            x_of[k] = load_batch(x_rows, k, "x_sb")
+
+        heads_of = {}
+        for k in range(BATCHES + 1):
+            if k + 1 < BATCHES:
+                packed_of[k + 1] = quantise_batch(grouped_of[k + 1])
+            if k < BATCHES:
+                heads_of[k] = heads_of_batch(packed_of[k][0], packed_of[k][1])
+            if k + 2 < BATCHES:
+                grouped_of[k + 2] = transpose_batch(xt_of[k + 2])
+            if k < BATCHES:
+                log_of_batch(heads_of[k][1])
+            if k >= 1:
+                blend_batch(k - 1, heads_of[k - 1][0], heads_of[k - 1][1], eps_of[k - 1], x_of[k - 1])
+                if k + 1 < BATCHES:
+                    eps_of[k + 1] = load_batch(eps_rows, k + 1, "eps_sb")
+                    x_of[k + 1] = load_batch(x_rows, k + 1, "x_sb")

@@ -24,6 +24,7 @@ BATCH = 4
 BATCHES = ROW_TILES // BATCH
 BANK = 512
 HALVES = FEATURES // BANK
+FEATURE_TILES = FEATURES // P
 WORDS = K_PASS // 2
 SPREAD, MEAN = 0, 1
 LN_FLOOR = 2.0**-60
@@ -44,10 +45,11 @@ def tile_diffscm_pb_kernel(
         const = ctx.enter_context(tc.tile_pool(name="const", bufs=1))
         loads = ctx.enter_context(tc.tile_pool(name="loads", bufs=2))
         regroup = ctx.enter_context(tc.tile_pool(name="regroup", bufs=1))
-        packed = ctx.enter_context(tc.tile_pool(name="packed", bufs=2))
+        packed = ctx.enter_context(tc.tile_pool(name="packed", bufs=BATCHES))
         work = ctx.enter_context(tc.tile_pool(name="work", bufs=2))
         flip_banks = ctx.enter_context(tc.psum_pool(name="flip_banks", bufs=2))
-        sum_banks = ctx.enter_context(tc.psum_pool(name="sum_banks", bufs=6))
+        sum_banks = ctx.enter_context(tc.psum_pool(name="sum_banks", bufs=4))
+        back_banks = ctx.enter_context(tc.psum_pool(name="back_banks", bufs=2))
         ctx.enter_context(tc.manual_schedule())
 
         def load_batch(source, k, label):
@@ -63,11 +65,14 @@ def tile_diffscm_pb_kernel(
         xt_of = {0: load_batch(xt_rows, 0, "xt_sb")}
 
         w_words = const.tile([P, 2, PASSES, 2 * FEATURES], U8, align_bytes=64)
-        for head, words, scales in ((SPREAD, Wv_words, Wv_scales), (MEAN, Wm_words, Wm_scales)):
+        for head, words, scale_rows in (
+            (SPREAD, Wv_words, Wv_scales),
+            (MEAN, Wm_words, Wm_scales),
+        ):
             for quadrant in range(4):
                 nc.sync.dma_start(
                     out=w_scales[32 * quadrant : 32 * quadrant + 4, head].bitcast(I32),
-                    in_=scales.bitcast(I32)[:, 4 * quadrant : 4 * quadrant + 4, :].rearrange(
+                    in_=scale_rows.bitcast(I32)[:, 4 * quadrant : 4 * quadrant + 4, :].rearrange(
                         "g r w -> r g w"
                     ),
                 )
@@ -76,11 +81,23 @@ def tile_diffscm_pb_kernel(
                 in_=words.bitcast(I32).rearrange("g p w -> p g w"),
             )
 
+        bv_square_bf = const.tile([P, P], BF16)
+        nc.vector.memset(bv_square_bf[:], 0.0)
+        nc.scalar.dma_start(
+            out=bv_square_bf[0:FEATURE_TILES, :], in_=bv.rearrange("(c n) -> c n", n=P)
+        )
         t_bf = const.tile([P, ROW_TILES], BF16)
         nc.scalar.dma_start(out=t_bf[:], in_=t_rand.rearrange("(p i) o -> p (i o)", i=ROW_TILES))
-        bias_rows = const.tile([P, 2, FEATURES], BF16)
-        nc.scalar.dma_start(out=bias_rows[:, SPREAD, :], in_=bv.partition_broadcast(P))
-        nc.scalar.dma_start(out=bias_rows[:, MEAN, :], in_=bm.partition_broadcast(P))
+        bm_rows = const.tile([P, FEATURES], BF16)
+        nc.scalar.dma_start(out=bm_rows[:], in_=bm.partition_broadcast(P))
+
+        bv_square = const.tile([P, P], F32)
+        nc.vector.tensor_copy(out=bv_square[:], in_=bv_square_bf[:])
+        bv_flipped = sum_banks.tile([P, BANK], F32, tag="sums")
+        nc.tensor.transpose(bv_flipped[:, 0:P], bv_square[:], identity[:])
+        bv_col = const.tile([P, FEATURE_TILES], F32)
+        nc.vector.tensor_copy(out=bv_col[:], in_=bv_flipped[:, 0:FEATURE_TILES])
+
         t_new = const.tile([P, ROW_TILES], F32)
         nc.vector.tensor_copy(out=t_new[:], in_=t_bf[:])
         t_old = const.tile([P, ROW_TILES], F32)
@@ -88,10 +105,10 @@ def tile_diffscm_pb_kernel(
             out=t_old[:], in0=t_bf[:], scalar1=-1.0, scalar2=1.0, op0=ALU.mult, op1=ALU.add
         )
 
-        def transpose_batch(xt_sb):
-            grouped = regroup.tile([P, BATCH * PASSES * P * PACK], BF16, align_bytes=64)
+        def quantise_batch(xt_sb):
+            grouped = regroup.tile([P, PASSES * BATCH * P * PACK], BF16, align_bytes=64)
             grouped_words = grouped[:].bitcast(F32).rearrange(
-                "p (i g r u) -> p i g r u", i=BATCH, g=PASSES, u=2
+                "p (g i r u) -> p g i r u", g=PASSES, i=BATCH, u=2
             )
             for i in range(BATCH):
                 row_words = xt_sb[:, i, :].bitcast(F32)
@@ -103,85 +120,103 @@ def tile_diffscm_pb_kernel(
                             row_words[:, WORDS * g + u : WORDS * (g + 1) : 2],
                             identity[:],
                         )
-                nc.scalar.copy(
-                    out=grouped_words[:, i], in_=flipped[:].rearrange("p g u r -> p g r u")
+                nc.vector.tensor_copy(
+                    out=grouped_words[:, :, i], in_=flipped[:].rearrange("p g u r -> p g r u")
                 )
-            return grouped
-
-        def quantise_batch(grouped):
-            codes = packed.tile([P, BATCH, PASSES, P], U32, align_bytes=64)
-            scales = packed.tile([P, BATCH, PASSES, P], U8, align_bytes=64)
+            codes = packed.tile([P, PASSES, BATCH, P], U32, align_bytes=64)
+            code_scales = packed.tile([P, PASSES, BATCH, P], U8, align_bytes=64)
             nc.vector.quantize_mx(
-                out=codes[:].rearrange("p i g r -> p (i g r)").bitcast(FP8X4),
-                scales=scales[:].rearrange("p i g r -> p (i g r)"),
+                out=codes[:].rearrange("p g i r -> p (g i r)").bitcast(FP8X4),
+                scales=code_scales[:].rearrange("p g i r -> p (g i r)"),
                 in_=grouped[:],
             )
-            return codes, scales
+            return codes, code_scales
 
-        def heads_of_batch(codes, scales):
-            pre = work.tile([P, 2, BATCH, FEATURES], F32)
-            gate = work.tile([P, BATCH, FEATURES], F32)
-            for i in range(BATCH):
-                for head in (SPREAD, MEAN):
-                    for half in range(HALVES):
-                        cols = slice(half * BANK, (half + 1) * BANK)
-                        sums = sum_banks.tile([P, BANK], F32)
-                        for g in range(PASSES):
-                            nc.tensor.matmul_mx(
-                                out=sums[:],
-                                lhsT=codes[:, i, g, :].bitcast(FP8X4),
-                                lhsT_scale=scales[:, i, g, :],
-                                rhs=w_words[
-                                    :, head, g, 2 * half * BANK : 2 * (half + 1) * BANK
-                                ].bitcast(FP4X4),
-                                rhs_scale=w_scales[:, head, g, cols],
-                                start=(g == 0),
-                                stop=(g == PASSES - 1),
-                            )
-                        nc.vector.tensor_tensor(
-                            out=pre[:, head, i, cols],
-                            in0=sums[:],
-                            in1=bias_rows[:, head, cols],
-                            op=ALU.add,
-                        )
+        def spread_of_batch(codes, code_scales):
+            v_flipped = work.tile([P, FEATURE_TILES, BATCH * P], F32)
+            for c in range(FEATURE_TILES):
+                sums = sum_banks.tile([P, BANK], F32, tag="sums")
+                for g in range(PASSES):
+                    nc.tensor.matmul_mx(
+                        out=sums[:],
+                        lhsT=w_words[:, SPREAD, g, 2 * c * P : 2 * (c + 1) * P].bitcast(FP4X4),
+                        lhsT_scale=w_scales[:, SPREAD, g, c * P : (c + 1) * P],
+                        rhs=codes[:, g].rearrange("p i r -> p (i r)").bitcast(FP8X4),
+                        rhs_scale=code_scales[:, g].rearrange("p i r -> p (i r)"),
+                        start=(g == 0),
+                        stop=(g == PASSES - 1),
+                    )
                 nc.scalar.activation(
-                    out=gate[:, i, :], in_=pre[:, SPREAD, i, :], func=ACT.Sigmoid, scale=-1.0
+                    out=v_flipped[:, c, :], in_=sums[:], func=ACT.Identity, bias=bv_col[:, c : c + 1]
                 )
-            return pre, gate
-
-        def log_of_batch(gate):
-            flat = gate[:].rearrange("p i n -> p (i n)")
-            nc.scalar.activation(out=flat, in_=flat, func=ACT.Ln, bias=LN_FLOOR)
-
-        def blend_batch(k, pre, gate, eps_sb, x_sb):
-            spread = pre[:, SPREAD].rearrange("p i n -> p (i n)")
-            nc.vector.scalar_tensor_tensor(
-                out=spread,
-                in0=gate[:].rearrange("p i n -> p (i n)"),
-                scalar=-1.0,
-                in1=spread,
-                op0=ALU.mult,
-                op1=ALU.max,
+            log_gate = work.tile([P, FEATURE_TILES * BATCH * P], F32)
+            nc.scalar.activation(
+                out=log_gate[:],
+                in_=v_flipped[:].rearrange("p c b -> p (c b)"),
+                func=ACT.Sigmoid,
+                scale=-1.0,
             )
+            nc.scalar.activation(out=log_gate[:], in_=log_gate[:], func=ACT.Ln, bias=LN_FLOOR)
+            return v_flipped, log_gate
+
+        def mean_of_batch(codes, code_scales):
+            mean = work.tile([P, BATCH, FEATURES], F32)
+            for i in range(BATCH):
+                for half in range(HALVES):
+                    cols = slice(half * BANK, (half + 1) * BANK)
+                    sums = sum_banks.tile([P, BANK], F32, tag="sums")
+                    for g in range(PASSES):
+                        nc.tensor.matmul_mx(
+                            out=sums[:],
+                            lhsT=codes[:, g, i, :].bitcast(FP8X4),
+                            lhsT_scale=code_scales[:, g, i, :],
+                            rhs=w_words[
+                                :, MEAN, g, 2 * half * BANK : 2 * (half + 1) * BANK
+                            ].bitcast(FP4X4),
+                            rhs_scale=w_scales[:, MEAN, g, cols],
+                            start=(g == 0),
+                            stop=(g == PASSES - 1),
+                        )
+                    nc.vector.tensor_tensor(
+                        out=mean[:, i, cols], in0=sums[:], in1=bm_rows[:, cols], op=ALU.add
+                    )
+            return mean
+
+        def softplus_of_batch(v_flipped, log_gate):
+            flat = v_flipped[:].rearrange("p c b -> p (c b)")
+            nc.vector.scalar_tensor_tensor(
+                out=flat, in0=log_gate[:], scalar=-1.0, in1=flat, op0=ALU.mult, op1=ALU.max
+            )
+
+        def blend_batch(k, sigma_flipped, mean, eps_sb, x_sb):
             result = work.tile([P, BATCH, FEATURES], F32)
             for step in range(BATCH + 2):
                 if step < BATCH:
                     i = step
-                    nc.vector.scalar_tensor_tensor(
-                        out=pre[:, SPREAD, i, :],
-                        in0=pre[:, SPREAD, i, :],
-                        scalar=t_new[:, k * BATCH + i : k * BATCH + i + 1],
-                        in1=eps_sb[:, i, :],
-                        op0=ALU.mult,
-                        op1=ALU.mult,
-                    )
+                    for half in range(HALVES):
+                        cols = slice(half * BANK, (half + 1) * BANK)
+                        sigma = back_banks.tile([P, BANK // P, P], F32)
+                        for q in range(BANK // P):
+                            nc.tensor.transpose(
+                                sigma[:, q, :],
+                                sigma_flipped[:, half * (BANK // P) + q, i * P : (i + 1) * P],
+                                identity[:],
+                            )
+                        nc.vector.scalar_tensor_tensor(
+                            out=result[:, i, cols],
+                            in0=sigma[:].rearrange("p q n -> p (q n)"),
+                            scalar=t_new[:, k * BATCH + i : k * BATCH + i + 1],
+                            in1=eps_sb[:, i, cols],
+                            op0=ALU.mult,
+                            op1=ALU.mult,
+                        )
                 if 0 <= step - 1 < BATCH:
                     i = step - 1
                     nc.vector.scalar_tensor_tensor(
-                        out=pre[:, MEAN, i, :],
-                        in0=pre[:, MEAN, i, :],
+                        out=mean[:, i, :],
+                        in0=mean[:, i, :],
                         scalar=t_new[:, k * BATCH + i : k * BATCH + i + 1],
-                        in1=pre[:, SPREAD, i, :],
+                        in1=result[:, i, :],
                         op0=ALU.mult,
                         op1=ALU.add,
                     )
@@ -191,36 +226,32 @@ def tile_diffscm_pb_kernel(
                         out=result[:, i, :],
                         in0=x_sb[:, i, :],
                         scalar=t_old[:, k * BATCH + i : k * BATCH + i + 1],
-                        in1=pre[:, MEAN, i, :],
+                        in1=mean[:, i, :],
                         op0=ALU.mult,
                         op1=ALU.add,
                     )
                     nc.sync.dma_start(out=out_rows[:, k * BATCH + i, :], in_=result[:, i, :])
 
-        xt_of[1] = load_batch(xt_rows, 1, "xt_sb")
-        grouped_of = {0: transpose_batch(xt_of[0])}
-        packed_of = {0: quantise_batch(grouped_of[0])}
-        xt_of[2] = load_batch(xt_rows, 2, "xt_sb")
-        grouped_of[1] = transpose_batch(xt_of[1])
-        xt_of[3] = load_batch(xt_rows, 3, "xt_sb")
+        packed_of = {}
+        for k in range(BATCHES):
+            if k + 1 < BATCHES:
+                xt_of[k + 1] = load_batch(xt_rows, k + 1, "xt_sb")
+            packed_of[k] = quantise_batch(xt_of[k])
+            if k == 1:
+                spread_of = {0: spread_of_batch(packed_of[0][0], packed_of[0][1])}
+                mean_of = {0: mean_of_batch(packed_of[0][0], packed_of[0][1])}
         eps_of = {}
         x_of = {}
         for k in range(2):
             eps_of[k] = load_batch(eps_rows, k, "eps_sb")
             x_of[k] = load_batch(x_rows, k, "x_sb")
 
-        heads_of = {}
-        for k in range(BATCHES + 1):
+        for k in range(1, BATCHES + 1):
+            if k < BATCHES:
+                mean_of[k] = mean_of_batch(packed_of[k][0], packed_of[k][1])
+                spread_of[k] = spread_of_batch(packed_of[k][0], packed_of[k][1])
+            softplus_of_batch(spread_of[k - 1][0], spread_of[k - 1][1])
+            blend_batch(k - 1, spread_of[k - 1][0], mean_of[k - 1], eps_of[k - 1], x_of[k - 1])
             if k + 1 < BATCHES:
-                packed_of[k + 1] = quantise_batch(grouped_of[k + 1])
-            if k < BATCHES:
-                heads_of[k] = heads_of_batch(packed_of[k][0], packed_of[k][1])
-            if k + 2 < BATCHES:
-                grouped_of[k + 2] = transpose_batch(xt_of[k + 2])
-            if k < BATCHES:
-                log_of_batch(heads_of[k][1])
-            if k >= 1:
-                blend_batch(k - 1, heads_of[k - 1][0], heads_of[k - 1][1], eps_of[k - 1], x_of[k - 1])
-                if k + 1 < BATCHES:
-                    eps_of[k + 1] = load_batch(eps_rows, k + 1, "eps_sb")
-                    x_of[k + 1] = load_batch(x_rows, k + 1, "x_sb")
+                eps_of[k + 1] = load_batch(eps_rows, k + 1, "eps_sb")
+                x_of[k + 1] = load_batch(x_rows, k + 1, "x_sb")

@@ -43,13 +43,13 @@ def tile_diffscm_pb_kernel(
 
     with ExitStack() as ctx:
         const = ctx.enter_context(tc.tile_pool(name="const", bufs=1))
+        xt_tiles = ctx.enter_context(tc.tile_pool(name="xt_tiles", bufs=2 * BATCH))
         loads = ctx.enter_context(tc.tile_pool(name="loads", bufs=2))
         regroup = ctx.enter_context(tc.tile_pool(name="regroup", bufs=1))
         packed = ctx.enter_context(tc.tile_pool(name="packed", bufs=BATCHES))
         work = ctx.enter_context(tc.tile_pool(name="work", bufs=2))
-        flip_banks = ctx.enter_context(tc.psum_pool(name="flip_banks", bufs=2))
+        flip_banks = ctx.enter_context(tc.psum_pool(name="flip_banks", bufs=4))
         sum_banks = ctx.enter_context(tc.psum_pool(name="sum_banks", bufs=4))
-        back_banks = ctx.enter_context(tc.psum_pool(name="back_banks", bufs=2))
         ctx.enter_context(tc.manual_schedule())
 
         def load_batch(source, k, label):
@@ -57,18 +57,22 @@ def tile_diffscm_pb_kernel(
             nc.sync.dma_start(out=rows[:], in_=source[:, k * BATCH : (k + 1) * BATCH, :])
             return rows
 
+        def load_xt_batch(k):
+            tiles = []
+            for i in range(BATCH):
+                xt_sb = xt_tiles.tile([P, FEATURES], BF16)
+                nc.sync.dma_start(out=xt_sb[:], in_=xt_rows[:, k * BATCH + i, :])
+                tiles.append(xt_sb)
+            return tiles
+
         w_scales = const.tile([P, 2, PASSES, FEATURES], U8, align_bytes=64)
         nc.vector.memset(w_scales[:].rearrange("p h g n -> p (h g n)").bitcast(I32), 0)
         identity = const.tile([P, P], F32)
         make_identity(nc, identity[:])
 
-        xt_of = {0: load_batch(xt_rows, 0, "xt_sb")}
-
         w_words = const.tile([P, 2, PASSES, 2 * FEATURES], U8, align_bytes=64)
-        for head, words, scale_rows in (
-            (SPREAD, Wv_words, Wv_scales),
-            (MEAN, Wm_words, Wm_scales),
-        ):
+
+        def load_weights(head, words, scale_rows):
             for quadrant in range(4):
                 nc.sync.dma_start(
                     out=w_scales[32 * quadrant : 32 * quadrant + 4, head].bitcast(I32),
@@ -81,6 +85,11 @@ def tile_diffscm_pb_kernel(
                 in_=words.bitcast(I32).rearrange("g p w -> p g w"),
             )
 
+        xt_of = {0: load_xt_batch(0)}
+        load_weights(SPREAD, Wv_words, Wv_scales)
+        xt_of[1] = load_xt_batch(1)
+        load_weights(MEAN, Wm_words, Wm_scales)
+
         bv_square_bf = const.tile([P, P], BF16)
         nc.vector.memset(bv_square_bf[:], 0.0)
         nc.scalar.dma_start(
@@ -90,6 +99,9 @@ def tile_diffscm_pb_kernel(
         nc.scalar.dma_start(out=t_bf[:], in_=t_rand.rearrange("(p i) o -> p (i o)", i=ROW_TILES))
         bm_rows = const.tile([P, FEATURES], BF16)
         nc.scalar.dma_start(out=bm_rows[:], in_=bm.partition_broadcast(P))
+        warm = const.tile([P, 1], F32)
+        nc.vector.memset(warm[:], 0.0)
+        nc.scalar.activation(out=warm[:], in_=warm[:], func=ACT.Sigmoid)
 
         bv_square = const.tile([P, P], F32)
         nc.vector.tensor_copy(out=bv_square[:], in_=bv_square_bf[:])
@@ -105,14 +117,14 @@ def tile_diffscm_pb_kernel(
             out=t_old[:], in0=t_bf[:], scalar1=-1.0, scalar2=1.0, op0=ALU.mult, op1=ALU.add
         )
 
-        def quantise_batch(xt_sb):
+        def quantise_batch(tiles):
             grouped = regroup.tile([P, PASSES * BATCH * P * PACK], BF16, align_bytes=64)
             grouped_words = grouped[:].bitcast(F32).rearrange(
                 "p (g i r u) -> p g i r u", g=PASSES, i=BATCH, u=2
             )
             for i in range(BATCH):
-                row_words = xt_sb[:, i, :].bitcast(F32)
-                flipped = flip_banks.tile([P, PASSES, 2, P], F32)
+                row_words = tiles[i][:].bitcast(F32)
+                flipped = flip_banks.tile([P, PASSES, 2, P], F32, tag="flip")
                 for g in range(PASSES):
                     for u in range(2):
                         nc.tensor.transpose(
@@ -159,28 +171,25 @@ def tile_diffscm_pb_kernel(
             nc.scalar.activation(out=log_gate[:], in_=log_gate[:], func=ACT.Ln, bias=LN_FLOOR)
             return v_flipped, log_gate
 
-        def mean_of_batch(codes, code_scales):
-            mean = work.tile([P, BATCH, FEATURES], F32)
-            for i in range(BATCH):
-                for half in range(HALVES):
-                    cols = slice(half * BANK, (half + 1) * BANK)
-                    sums = sum_banks.tile([P, BANK], F32, tag="sums")
-                    for g in range(PASSES):
-                        nc.tensor.matmul_mx(
-                            out=sums[:],
-                            lhsT=codes[:, g, i, :].bitcast(FP8X4),
-                            lhsT_scale=code_scales[:, g, i, :],
-                            rhs=w_words[
-                                :, MEAN, g, 2 * half * BANK : 2 * (half + 1) * BANK
-                            ].bitcast(FP4X4),
-                            rhs_scale=w_scales[:, MEAN, g, cols],
-                            start=(g == 0),
-                            stop=(g == PASSES - 1),
-                        )
-                    nc.vector.tensor_tensor(
-                        out=mean[:, i, cols], in0=sums[:], in1=bm_rows[:, cols], op=ALU.add
+        def mean_of_tile(codes, code_scales, mean, i):
+            for half in range(HALVES):
+                cols = slice(half * BANK, (half + 1) * BANK)
+                sums = sum_banks.tile([P, BANK], F32, tag="sums")
+                for g in range(PASSES):
+                    nc.tensor.matmul_mx(
+                        out=sums[:],
+                        lhsT=codes[:, g, i, :].bitcast(FP8X4),
+                        lhsT_scale=code_scales[:, g, i, :],
+                        rhs=w_words[:, MEAN, g, 2 * half * BANK : 2 * (half + 1) * BANK].bitcast(
+                            FP4X4
+                        ),
+                        rhs_scale=w_scales[:, MEAN, g, cols],
+                        start=(g == 0),
+                        stop=(g == PASSES - 1),
                     )
-            return mean
+                nc.vector.tensor_tensor(
+                    out=mean[:, i, cols], in0=sums[:], in1=bm_rows[:, cols], op=ALU.add
+                )
 
         def softplus_of_batch(v_flipped, log_gate):
             flat = v_flipped[:].rearrange("p c b -> p (c b)")
@@ -188,58 +197,58 @@ def tile_diffscm_pb_kernel(
                 out=flat, in0=log_gate[:], scalar=-1.0, in1=flat, op0=ALU.mult, op1=ALU.max
             )
 
-        def blend_batch(k, sigma_flipped, mean, eps_sb, x_sb):
-            result = work.tile([P, BATCH, FEATURES], F32)
-            for step in range(BATCH + 2):
-                if step < BATCH:
-                    i = step
-                    for half in range(HALVES):
-                        cols = slice(half * BANK, (half + 1) * BANK)
-                        sigma = back_banks.tile([P, BANK // P, P], F32)
-                        for q in range(BANK // P):
-                            nc.tensor.transpose(
-                                sigma[:, q, :],
-                                sigma_flipped[:, half * (BANK // P) + q, i * P : (i + 1) * P],
-                                identity[:],
-                            )
-                        nc.vector.scalar_tensor_tensor(
-                            out=result[:, i, cols],
-                            in0=sigma[:].rearrange("p q n -> p (q n)"),
-                            scalar=t_new[:, k * BATCH + i : k * BATCH + i + 1],
-                            in1=eps_sb[:, i, cols],
-                            op0=ALU.mult,
-                            op1=ALU.mult,
-                        )
-                if 0 <= step - 1 < BATCH:
-                    i = step - 1
-                    nc.vector.scalar_tensor_tensor(
-                        out=mean[:, i, :],
-                        in0=mean[:, i, :],
-                        scalar=t_new[:, k * BATCH + i : k * BATCH + i + 1],
-                        in1=result[:, i, :],
-                        op0=ALU.mult,
-                        op1=ALU.add,
+        def noise_of_tile(k, i, sigma_flipped, eps_sb, result):
+            for half in range(HALVES):
+                cols = slice(half * BANK, (half + 1) * BANK)
+                sigma = flip_banks.tile([P, BANK // P, P], F32, tag="flip")
+                for q in range(BANK // P):
+                    nc.tensor.transpose(
+                        sigma[:, q, :],
+                        sigma_flipped[:, half * (BANK // P) + q, i * P : (i + 1) * P],
+                        identity[:],
                     )
-                if 0 <= step - 2:
-                    i = step - 2
-                    nc.vector.scalar_tensor_tensor(
-                        out=result[:, i, :],
-                        in0=x_sb[:, i, :],
-                        scalar=t_old[:, k * BATCH + i : k * BATCH + i + 1],
-                        in1=mean[:, i, :],
-                        op0=ALU.mult,
-                        op1=ALU.add,
-                    )
-                    nc.sync.dma_start(out=out_rows[:, k * BATCH + i, :], in_=result[:, i, :])
+                nc.vector.scalar_tensor_tensor(
+                    out=result[:, i, cols],
+                    in0=sigma[:].rearrange("p q n -> p (q n)"),
+                    scalar=t_new[:, k * BATCH + i : k * BATCH + i + 1],
+                    in1=eps_sb[:, i, cols],
+                    op0=ALU.mult,
+                    op1=ALU.mult,
+                )
 
-        packed_of = {}
-        for k in range(BATCHES):
+        def sample_of_tile(k, i, mean, result):
+            nc.vector.scalar_tensor_tensor(
+                out=mean[:, i, :],
+                in0=mean[:, i, :],
+                scalar=t_new[:, k * BATCH + i : k * BATCH + i + 1],
+                in1=result[:, i, :],
+                op0=ALU.mult,
+                op1=ALU.add,
+            )
+
+        def blend_of_tile(k, i, mean, x_sb, result):
+            nc.vector.scalar_tensor_tensor(
+                out=result[:, i, :],
+                in0=x_sb[:, i, :],
+                scalar=t_old[:, k * BATCH + i : k * BATCH + i + 1],
+                in1=mean[:, i, :],
+                op0=ALU.mult,
+                op1=ALU.add,
+            )
+            nc.sync.dma_start(out=out_rows[:, k * BATCH + i, :], in_=result[:, i, :])
+
+        packed_of = {0: quantise_batch(xt_of[0])}
+        spread_of = {0: spread_of_batch(packed_of[0][0], packed_of[0][1])}
+        mean_of = {}
+        for k in range(1, BATCHES):
             if k + 1 < BATCHES:
-                xt_of[k + 1] = load_batch(xt_rows, k + 1, "xt_sb")
+                xt_of[k + 1] = load_xt_batch(k + 1)
             packed_of[k] = quantise_batch(xt_of[k])
             if k == 1:
-                spread_of = {0: spread_of_batch(packed_of[0][0], packed_of[0][1])}
-                mean_of = {0: mean_of_batch(packed_of[0][0], packed_of[0][1])}
+                mean = work.tile([P, BATCH, FEATURES], F32)
+                mean_of[0] = mean
+                for i in range(BATCH):
+                    mean_of_tile(packed_of[0][0], packed_of[0][1], mean, i)
         eps_of = {}
         x_of = {}
         for k in range(2):
@@ -248,10 +257,20 @@ def tile_diffscm_pb_kernel(
 
         for k in range(1, BATCHES + 1):
             if k < BATCHES:
-                mean_of[k] = mean_of_batch(packed_of[k][0], packed_of[k][1])
                 spread_of[k] = spread_of_batch(packed_of[k][0], packed_of[k][1])
+                mean = work.tile([P, BATCH, FEATURES], F32)
+                mean_of[k] = mean
             softplus_of_batch(spread_of[k - 1][0], spread_of[k - 1][1])
-            blend_batch(k - 1, spread_of[k - 1][0], mean_of[k - 1], eps_of[k - 1], x_of[k - 1])
+            result = work.tile([P, BATCH, FEATURES], F32)
+            for step in range(BATCH + 2):
+                if step < BATCH:
+                    if k < BATCHES:
+                        mean_of_tile(packed_of[k][0], packed_of[k][1], mean_of[k], step)
+                    noise_of_tile(k - 1, step, spread_of[k - 1][0], eps_of[k - 1], result)
+                if 0 <= step - 1 < BATCH:
+                    sample_of_tile(k - 1, step - 1, mean_of[k - 1], result)
+                if 0 <= step - 2:
+                    blend_of_tile(k - 1, step - 2, mean_of[k - 1], x_of[k - 1], result)
             if k + 1 < BATCHES:
                 eps_of[k + 1] = load_batch(eps_rows, k + 1, "eps_sb")
                 x_of[k + 1] = load_batch(x_rows, k + 1, "x_sb")

@@ -85,10 +85,11 @@ def tile_diffscm_pb_kernel(
                 in_=words.bitcast(I32).rearrange("g p w -> p g w"),
             )
 
-        xt_of = {0: load_xt_batch(0)}
+        xt_of = {0: load_xt_batch(0), 1: load_xt_batch(1)}
         load_weights(SPREAD, Wv_words, Wv_scales)
-        xt_of[1] = load_xt_batch(1)
         load_weights(MEAN, Wm_words, Wm_scales)
+        bm_rows = const.tile([P, FEATURES], BF16)
+        nc.sync.dma_start(out=bm_rows[:], in_=bm.partition_broadcast(P))
 
         bv_square_bf = const.tile([P, P], BF16)
         nc.vector.memset(bv_square_bf[:], 0.0)
@@ -97,18 +98,13 @@ def tile_diffscm_pb_kernel(
         )
         t_bf = const.tile([P, ROW_TILES], BF16)
         nc.scalar.dma_start(out=t_bf[:], in_=t_rand.rearrange("(p i) o -> p (i o)", i=ROW_TILES))
-        bm_rows = const.tile([P, FEATURES], BF16)
-        nc.scalar.dma_start(out=bm_rows[:], in_=bm.partition_broadcast(P))
         warm = const.tile([P, 1], F32)
         nc.vector.memset(warm[:], 0.0)
         nc.scalar.activation(out=warm[:], in_=warm[:], func=ACT.Sigmoid)
 
         bv_square = const.tile([P, P], F32)
         nc.vector.tensor_copy(out=bv_square[:], in_=bv_square_bf[:])
-        bv_flipped = sum_banks.tile([P, BANK], F32, tag="sums")
-        nc.tensor.transpose(bv_flipped[:, 0:P], bv_square[:], identity[:])
         bv_col = const.tile([P, FEATURE_TILES], F32)
-        nc.vector.tensor_copy(out=bv_col[:], in_=bv_flipped[:, 0:FEATURE_TILES])
 
         t_new = const.tile([P, ROW_TILES], F32)
         nc.vector.tensor_copy(out=t_new[:], in_=t_bf[:])
@@ -238,17 +234,19 @@ def tile_diffscm_pb_kernel(
             nc.sync.dma_start(out=out_rows[:, k * BATCH + i, :], in_=result[:, i, :])
 
         packed_of = {0: quantise_batch(xt_of[0])}
+        bv_flipped = sum_banks.tile([P, BANK], F32, tag="sums")
+        nc.tensor.transpose(bv_flipped[:, 0:P], bv_square[:], identity[:])
+        nc.vector.tensor_copy(out=bv_col[:], in_=bv_flipped[:, 0:FEATURE_TILES])
+        xt_of[2] = load_xt_batch(2)
+        packed_of[1] = quantise_batch(xt_of[1])
+        xt_of[3] = load_xt_batch(3)
         spread_of = {0: spread_of_batch(packed_of[0][0], packed_of[0][1])}
-        mean_of = {}
-        for k in range(1, BATCHES):
-            if k + 1 < BATCHES:
-                xt_of[k + 1] = load_xt_batch(k + 1)
-            packed_of[k] = quantise_batch(xt_of[k])
-            if k == 1:
-                mean = work.tile([P, BATCH, FEATURES], F32)
-                mean_of[0] = mean
-                for i in range(BATCH):
-                    mean_of_tile(packed_of[0][0], packed_of[0][1], mean, i)
+        mean = work.tile([P, BATCH, FEATURES], F32)
+        mean_of = {0: mean}
+        for i in range(BATCH):
+            mean_of_tile(packed_of[0][0], packed_of[0][1], mean, i)
+        packed_of[2] = quantise_batch(xt_of[2])
+        packed_of[3] = quantise_batch(xt_of[3])
         eps_of = {}
         x_of = {}
         for k in range(2):

@@ -29,6 +29,8 @@ WORDS = K_PASS // 2
 SPREAD, MEAN = 0, 1
 LN_FLOOR = 2.0**-60
 
+GROUPS = ((0, 0, 2), (0, 2, 8), (1, 0, 8), (2, 0, 8), (3, 0, 6), (3, 6, 8))
+
 FLOPS = 2 * ROWS * FEATURES * 2 * FEATURES
 
 
@@ -43,25 +45,28 @@ def tile_diffscm_pb_kernel(
 
     with ExitStack() as ctx:
         const = ctx.enter_context(tc.tile_pool(name="const", bufs=1))
-        xt_tiles = ctx.enter_context(tc.tile_pool(name="xt_tiles", bufs=2 * BATCH))
+        xt_tiles = ctx.enter_context(tc.tile_pool(name="xt_tiles", bufs=ROW_TILES))
         loads = ctx.enter_context(tc.tile_pool(name="loads", bufs=2))
-        regroup = ctx.enter_context(tc.tile_pool(name="regroup", bufs=1))
+        regroup = ctx.enter_context(tc.tile_pool(name="regroup", bufs=2))
         packed = ctx.enter_context(tc.tile_pool(name="packed", bufs=BATCHES))
-        work = ctx.enter_context(tc.tile_pool(name="work", bufs=2))
+        samples = ctx.enter_context(tc.tile_pool(name="samples", bufs=3))
+        gates = ctx.enter_context(tc.tile_pool(name="gates", bufs=2))
+        blends = ctx.enter_context(tc.tile_pool(name="blends", bufs=2))
         flip_banks = ctx.enter_context(tc.psum_pool(name="flip_banks", bufs=4))
-        sum_banks = ctx.enter_context(tc.psum_pool(name="sum_banks", bufs=4))
+        spread_banks = ctx.enter_context(tc.psum_pool(name="spread_banks", bufs=2))
+        mean_banks = ctx.enter_context(tc.psum_pool(name="mean_banks", bufs=2))
         ctx.enter_context(tc.manual_schedule())
 
-        def load_batch(source, k, label):
+        def load_batch(source, b, label):
             rows = loads.tile([P, BATCH, FEATURES], BF16, name=label, tag=label)
-            nc.sync.dma_start(out=rows[:], in_=source[:, k * BATCH : (k + 1) * BATCH, :])
+            nc.sync.dma_start(out=rows[:], in_=source[:, b * BATCH : (b + 1) * BATCH, :])
             return rows
 
-        def load_xt_batch(k):
+        def load_xt_batch(b):
             tiles = []
             for i in range(BATCH):
                 xt_sb = xt_tiles.tile([P, FEATURES], BF16)
-                nc.sync.dma_start(out=xt_sb[:], in_=xt_rows[:, k * BATCH + i, :])
+                nc.sync.dma_start(out=xt_sb[:], in_=xt_rows[:, b * BATCH + i, :])
                 tiles.append(xt_sb)
             return tiles
 
@@ -69,6 +74,8 @@ def tile_diffscm_pb_kernel(
         nc.vector.memset(w_scales[:].rearrange("p h g n -> p (h g n)").bitcast(I32), 0)
         identity = const.tile([P, P], F32)
         make_identity(nc, identity[:])
+        identity_bf = const.tile([P, P], BF16)
+        make_identity(nc, identity_bf[:])
 
         w_words = const.tile([P, 2, PASSES, 2 * FEATURES], U8, align_bytes=64)
 
@@ -85,16 +92,25 @@ def tile_diffscm_pb_kernel(
                 in_=words.bitcast(I32).rearrange("g p w -> p g w"),
             )
 
-        xt_of = {0: load_xt_batch(0), 1: load_xt_batch(1)}
+        xt_of = {0: load_xt_batch(0)}
         load_weights(SPREAD, Wv_words, Wv_scales)
         load_weights(MEAN, Wm_words, Wm_scales)
-        bm_rows = const.tile([P, FEATURES], BF16)
-        nc.sync.dma_start(out=bm_rows[:], in_=bm.partition_broadcast(P))
+        eps_of = {0: load_batch(eps_rows, 0, "eps_sb")}
+        xt_of[1] = load_xt_batch(1)
+        xt_of[2] = load_xt_batch(2)
+        x_of = {0: load_batch(x_rows, 0, "x_sb")}
+        xt_of[3] = load_xt_batch(3)
+        eps_of[1] = load_batch(eps_rows, 1, "eps_sb")
+        x_of[1] = load_batch(x_rows, 1, "x_sb")
 
-        bv_square_bf = const.tile([P, P], BF16)
-        nc.vector.memset(bv_square_bf[:], 0.0)
+        bias_square_bf = const.tile([P, P], BF16)
+        nc.vector.memset(bias_square_bf[:], 0.0)
         nc.scalar.dma_start(
-            out=bv_square_bf[0:FEATURE_TILES, :], in_=bv.rearrange("(c n) -> c n", n=P)
+            out=bias_square_bf[0:FEATURE_TILES, :], in_=bv.rearrange("(c n) -> c n", n=P)
+        )
+        nc.scalar.dma_start(
+            out=bias_square_bf[FEATURE_TILES : 2 * FEATURE_TILES, :],
+            in_=bm.rearrange("(c n) -> c n", n=P),
         )
         t_bf = const.tile([P, ROW_TILES], BF16)
         nc.scalar.dma_start(out=t_bf[:], in_=t_rand.rearrange("(p i) o -> p (i o)", i=ROW_TILES))
@@ -102,9 +118,9 @@ def tile_diffscm_pb_kernel(
         nc.vector.memset(warm[:], 0.0)
         nc.scalar.activation(out=warm[:], in_=warm[:], func=ACT.Sigmoid)
 
-        bv_square = const.tile([P, P], F32)
-        nc.vector.tensor_copy(out=bv_square[:], in_=bv_square_bf[:])
-        bv_col = const.tile([P, FEATURE_TILES], F32)
+        bias_square = const.tile([P, P], F32)
+        nc.vector.tensor_copy(out=bias_square[:], in_=bias_square_bf[:])
+        bias_col = const.tile([P, 2 * FEATURE_TILES], F32)
 
         t_new = const.tile([P, ROW_TILES], F32)
         nc.vector.tensor_copy(out=t_new[:], in_=t_bf[:])
@@ -113,13 +129,13 @@ def tile_diffscm_pb_kernel(
             out=t_old[:], in0=t_bf[:], scalar1=-1.0, scalar2=1.0, op0=ALU.mult, op1=ALU.add
         )
 
-        def quantise_batch(tiles):
+        def flip_xt(b):
             grouped = regroup.tile([P, PASSES * BATCH * P * PACK], BF16, align_bytes=64)
             grouped_words = grouped[:].bitcast(F32).rearrange(
                 "p (g i r u) -> p g i r u", g=PASSES, i=BATCH, u=2
             )
             for i in range(BATCH):
-                row_words = tiles[i][:].bitcast(F32)
+                row_words = xt_of[b][i][:].bitcast(F32)
                 flipped = flip_banks.tile([P, PASSES, 2, P], F32, tag="flip")
                 for g in range(PASSES):
                     for u in range(2):
@@ -131,6 +147,9 @@ def tile_diffscm_pb_kernel(
                 nc.vector.tensor_copy(
                     out=grouped_words[:, :, i], in_=flipped[:].rearrange("p g u r -> p g r u")
                 )
+            return grouped
+
+        def quantise(grouped):
             codes = packed.tile([P, PASSES, BATCH, P], U32, align_bytes=64)
             code_scales = packed.tile([P, PASSES, BATCH, P], U8, align_bytes=64)
             nc.vector.quantize_mx(
@@ -140,135 +159,225 @@ def tile_diffscm_pb_kernel(
             )
             return codes, code_scales
 
-        def spread_of_batch(codes, code_scales):
-            v_flipped = work.tile([P, FEATURE_TILES, BATCH * P], F32)
-            for c in range(FEATURE_TILES):
-                sums = sum_banks.tile([P, BANK], F32, tag="sums")
-                for g in range(PASSES):
-                    nc.tensor.matmul_mx(
-                        out=sums[:],
-                        lhsT=w_words[:, SPREAD, g, 2 * c * P : 2 * (c + 1) * P].bitcast(FP4X4),
-                        lhsT_scale=w_scales[:, SPREAD, g, c * P : (c + 1) * P],
-                        rhs=codes[:, g].rearrange("p i r -> p (i r)").bitcast(FP8X4),
-                        rhs_scale=code_scales[:, g].rearrange("p i r -> p (i r)"),
-                        start=(g == 0),
-                        stop=(g == PASSES - 1),
-                    )
-                nc.scalar.activation(
-                    out=v_flipped[:, c, :], in_=sums[:], func=ACT.Identity, bias=bv_col[:, c : c + 1]
+        packed_of = {}
+        sample_of = {}
+        gate_of = {}
+        blend_of = {}
+
+        def product(bank, head, b, c):
+            codes, code_scales = packed_of[b]
+            for g in range(PASSES):
+                nc.tensor.matmul_mx(
+                    out=bank[:],
+                    lhsT=w_words[:, head, g, 2 * c * P : 2 * (c + 1) * P].bitcast(FP4X4),
+                    lhsT_scale=w_scales[:, head, g, c * P : (c + 1) * P],
+                    rhs=codes[:, g].rearrange("p i r -> p (i r)").bitcast(FP8X4),
+                    rhs_scale=code_scales[:, g].rearrange("p i r -> p (i r)"),
+                    start=(g == 0),
+                    stop=(g == PASSES - 1),
                 )
-            log_gate = work.tile([P, FEATURE_TILES * BATCH * P], F32)
+
+        def spread_of_group(group, on_vector):
+            b, first, end = group
+            if b not in sample_of:
+                sample = samples.tile([P, FEATURE_TILES, BATCH * P], F32)
+                sample_of[b] = sample
+            for c in range(first, end):
+                sums = spread_banks.tile([P, BANK], F32, tag="spread")
+                product(sums, SPREAD, b, c)
+                if on_vector:
+                    nc.vector.tensor_scalar_add(
+                        out=sample_of[b][:, c, :], in0=sums[:], scalar1=bias_col[:, c : c + 1]
+                    )
+                else:
+                    nc.scalar.activation(
+                        out=sample_of[b][:, c, :],
+                        in_=sums[:],
+                        func=ACT.Identity,
+                        bias=bias_col[:, c : c + 1],
+                    )
+
+        def stretch(tile_, first, end):
+            return tile_[:, first:end, :].rearrange("p c b -> p (c b)")
+
+        def gate_of_group(group):
+            b, first, end = group
+            if b not in gate_of:
+                log_gate = gates.tile([P, FEATURE_TILES, BATCH * P], F32)
+                gate_of[b] = log_gate
             nc.scalar.activation(
-                out=log_gate[:],
-                in_=v_flipped[:].rearrange("p c b -> p (c b)"),
+                out=stretch(gate_of[b], first, end),
+                in_=stretch(sample_of[b], first, end),
                 func=ACT.Sigmoid,
                 scale=-1.0,
             )
-            nc.scalar.activation(out=log_gate[:], in_=log_gate[:], func=ACT.Ln, bias=LN_FLOOR)
-            return v_flipped, log_gate
-
-        def mean_of_tile(codes, code_scales, mean, i):
-            for half in range(HALVES):
-                cols = slice(half * BANK, (half + 1) * BANK)
-                sums = sum_banks.tile([P, BANK], F32, tag="sums")
-                for g in range(PASSES):
-                    nc.tensor.matmul_mx(
-                        out=sums[:],
-                        lhsT=codes[:, g, i, :].bitcast(FP8X4),
-                        lhsT_scale=code_scales[:, g, i, :],
-                        rhs=w_words[:, MEAN, g, 2 * half * BANK : 2 * (half + 1) * BANK].bitcast(
-                            FP4X4
-                        ),
-                        rhs_scale=w_scales[:, MEAN, g, cols],
-                        start=(g == 0),
-                        stop=(g == PASSES - 1),
-                    )
-                nc.vector.tensor_tensor(
-                    out=mean[:, i, cols], in0=sums[:], in1=bm_rows[:, cols], op=ALU.add
-                )
-
-        def softplus_of_batch(v_flipped, log_gate):
-            flat = v_flipped[:].rearrange("p c b -> p (c b)")
-            nc.vector.scalar_tensor_tensor(
-                out=flat, in0=log_gate[:], scalar=-1.0, in1=flat, op0=ALU.mult, op1=ALU.max
+            nc.scalar.activation(
+                out=stretch(gate_of[b], first, end),
+                in_=stretch(gate_of[b], first, end),
+                func=ACT.Ln,
+                bias=LN_FLOOR,
             )
 
-        def noise_of_tile(k, i, sigma_flipped, eps_sb, result):
-            for half in range(HALVES):
-                cols = slice(half * BANK, (half + 1) * BANK)
-                sigma = flip_banks.tile([P, BANK // P, P], F32, tag="flip")
-                for q in range(BANK // P):
+        def softplus_of_group(group):
+            b, first, end = group
+            nc.vector.scalar_tensor_tensor(
+                out=stretch(sample_of[b], first, end),
+                in0=stretch(gate_of[b], first, end),
+                scalar=-1.0,
+                in1=stretch(sample_of[b], first, end),
+                op0=ALU.mult,
+                op1=ALU.max,
+            )
+
+        def flip_eps(b, pair):
+            eps_flipped = flip_banks.tile([P, 2, BATCH, P], BF16, tag="flip")
+            for side in range(2):
+                c = 2 * pair + side
+                for i in range(BATCH):
                     nc.tensor.transpose(
-                        sigma[:, q, :],
-                        sigma_flipped[:, half * (BANK // P) + q, i * P : (i + 1) * P],
-                        identity[:],
+                        eps_flipped[:, side, i, :],
+                        eps_of[b][:, i, c * P : (c + 1) * P],
+                        identity_bf[:],
                     )
-                nc.vector.scalar_tensor_tensor(
-                    out=result[:, i, cols],
-                    in0=sigma[:].rearrange("p q n -> p (q n)"),
-                    scalar=t_new[:, k * BATCH + i : k * BATCH + i + 1],
-                    in1=eps_sb[:, i, cols],
+            return eps_flipped
+
+        def noise_of_pair(b, pair, eps_flipped):
+            nc.vector.tensor_tensor(
+                out=stretch(sample_of[b], 2 * pair, 2 * pair + 2),
+                in0=stretch(sample_of[b], 2 * pair, 2 * pair + 2),
+                in1=eps_flipped[:].rearrange("p s i r -> p (s i r)"),
+                op=ALU.mult,
+            )
+
+        def mean_product(b, c):
+            sums = mean_banks.tile([P, BANK], F32, tag="mean")
+            product(sums, MEAN, b, c)
+            return sums
+
+        def sample_of_tile(b, c, sums):
+            nc.vector.scalar_tensor_tensor(
+                out=sample_of[b][:, c, :],
+                in0=sums[:],
+                scalar=bias_col[:, FEATURE_TILES + c : FEATURE_TILES + c + 1],
+                in1=sample_of[b][:, c, :],
+                op0=ALU.add,
+                op1=ALU.add,
+            )
+
+        def old_share(b):
+            blend = blends.tile([P, BATCH, FEATURES], F32)
+            blend_of[b] = blend
+            for i in range(BATCH):
+                nc.gpsimd.tensor_scalar(
+                    out=blend[:, i, :],
+                    in0=x_of[b][:, i, :],
+                    scalar1=t_old[:, b * BATCH + i : b * BATCH + i + 1],
+                    scalar2=0.0,
                     op0=ALU.mult,
-                    op1=ALU.mult,
+                    op1=ALU.add,
                 )
 
-        def sample_of_tile(k, i, mean, result):
+        def flip_sample(b, i, half):
+            flipped = flip_banks.tile([P, BANK // P, P], F32, tag="flip")
+            for q in range(BANK // P):
+                nc.tensor.transpose(
+                    flipped[:, q, :],
+                    sample_of[b][:, half * (BANK // P) + q, i * P : (i + 1) * P],
+                    identity[:],
+                )
+            return flipped
+
+        def blend_half(b, i, half, flipped):
+            cols = slice(half * BANK, (half + 1) * BANK)
             nc.vector.scalar_tensor_tensor(
-                out=mean[:, i, :],
-                in0=mean[:, i, :],
-                scalar=t_new[:, k * BATCH + i : k * BATCH + i + 1],
-                in1=result[:, i, :],
+                out=blend_of[b][:, i, cols],
+                in0=flipped[:].rearrange("p q n -> p (q n)"),
+                scalar=t_new[:, b * BATCH + i : b * BATCH + i + 1],
+                in1=blend_of[b][:, i, cols],
                 op0=ALU.mult,
                 op1=ALU.add,
             )
 
-        def blend_of_tile(k, i, mean, x_sb, result):
-            nc.vector.scalar_tensor_tensor(
-                out=result[:, i, :],
-                in0=x_sb[:, i, :],
-                scalar=t_old[:, k * BATCH + i : k * BATCH + i + 1],
-                in1=mean[:, i, :],
-                op0=ALU.mult,
-                op1=ALU.add,
-            )
-            nc.sync.dma_start(out=out_rows[:, k * BATCH + i, :], in_=result[:, i, :])
+        def finish_batch(b):
+            order = [(i, half) for i in range(BATCH) for half in range(HALVES)]
+            ahead = 4
+            flipped_of = {}
+            for n in range(ahead):
+                flipped_of[order[n]] = flip_sample(b, order[n][0], order[n][1])
+            for n in range(len(order)):
+                i, half = order[n]
+                blend_half(b, i, half, flipped_of[order[n]])
+                if half == HALVES - 1:
+                    nc.sync.dma_start(out=out_rows[:, b * BATCH + i, :], in_=blend_of[b][:, i, :])
+                if n + ahead < len(order):
+                    later = order[n + ahead]
+                    flipped_of[later] = flip_sample(b, later[0], later[1])
 
-        packed_of = {0: quantise_batch(xt_of[0])}
-        bv_flipped = sum_banks.tile([P, BANK], F32, tag="sums")
-        nc.tensor.transpose(bv_flipped[:, 0:P], bv_square[:], identity[:])
-        nc.vector.tensor_copy(out=bv_col[:], in_=bv_flipped[:, 0:FEATURE_TILES])
-        xt_of[2] = load_xt_batch(2)
-        packed_of[1] = quantise_batch(xt_of[1])
-        xt_of[3] = load_xt_batch(3)
-        spread_of = {0: spread_of_batch(packed_of[0][0], packed_of[0][1])}
-        mean = work.tile([P, BATCH, FEATURES], F32)
-        mean_of = {0: mean}
-        for i in range(BATCH):
-            mean_of_tile(packed_of[0][0], packed_of[0][1], mean, i)
-        packed_of[2] = quantise_batch(xt_of[2])
-        packed_of[3] = quantise_batch(xt_of[3])
-        eps_of = {}
-        x_of = {}
-        for k in range(2):
-            eps_of[k] = load_batch(eps_rows, k, "eps_sb")
-            x_of[k] = load_batch(x_rows, k, "x_sb")
+        eps_ready = {}
+        mean_ready = {}
 
-        for k in range(1, BATCHES + 1):
-            if k < BATCHES:
-                spread_of[k] = spread_of_batch(packed_of[k][0], packed_of[k][1])
-                mean = work.tile([P, BATCH, FEATURES], F32)
-                mean_of[k] = mean
-            softplus_of_batch(spread_of[k - 1][0], spread_of[k - 1][1])
-            result = work.tile([P, BATCH, FEATURES], F32)
-            for step in range(BATCH + 2):
-                if step < BATCH:
-                    if k < BATCHES:
-                        mean_of_tile(packed_of[k][0], packed_of[k][1], mean_of[k], step)
-                    noise_of_tile(k - 1, step, spread_of[k - 1][0], eps_of[k - 1], result)
-                if 0 <= step - 1 < BATCH:
-                    sample_of_tile(k - 1, step - 1, mean_of[k - 1], result)
-                if 0 <= step - 2:
-                    blend_of_tile(k - 1, step - 2, mean_of[k - 1], x_of[k - 1], result)
-            if k + 1 < BATCHES:
-                eps_of[k + 1] = load_batch(eps_rows, k + 1, "eps_sb")
-                x_of[k + 1] = load_batch(x_rows, k + 1, "x_sb")
+        def pairs_of(group):
+            return list(range(group[1] // 2, group[2] // 2))
+
+        def prefill(group):
+            b = group[0]
+            pairs = pairs_of(group)
+            for pair in pairs[0:2]:
+                eps_ready[(b, pair)] = flip_eps(b, pair)
+            for side in range(2):
+                c = 2 * pairs[0] + side
+                mean_ready[(b, c)] = mean_product(b, c)
+
+        def body(group):
+            b = group[0]
+            pairs = pairs_of(group)
+            noise_of_pair(b, pairs[0], eps_ready[(b, pairs[0])])
+            for j in range(len(pairs)):
+                pair = pairs[j]
+                if j + 2 < len(pairs):
+                    eps_ready[(b, pairs[j + 2])] = flip_eps(b, pairs[j + 2])
+                if j + 1 < len(pairs):
+                    noise_of_pair(b, pairs[j + 1], eps_ready[(b, pairs[j + 1])])
+                for side in range(2):
+                    c = 2 * pair + side
+                    sample_of_tile(b, c, mean_ready[(b, c)])
+                    if j + 1 < len(pairs):
+                        later = 2 * pairs[j + 1] + side
+                        mean_ready[(b, later)] = mean_product(b, later)
+
+        packed_of[0] = quantise(flip_xt(0))
+        bias_flipped = flip_banks.tile([P, P], F32, tag="flip")
+        nc.tensor.transpose(bias_flipped[:], bias_square[:], identity[:])
+        nc.vector.tensor_copy(out=bias_col[:], in_=bias_flipped[:, 0 : 2 * FEATURE_TILES])
+
+        spread_of_group(GROUPS[0], False)
+        gate_of_group(GROUPS[0])
+        spread_of_group(GROUPS[1], True)
+        gate_of_group(GROUPS[1])
+        old_share(0)
+        prefill(GROUPS[0])
+
+        for n in range(len(GROUPS)):
+            group = GROUPS[n]
+            b = group[0]
+            softplus_of_group(group)
+            if n >= 1 and n + 1 < len(GROUPS):
+                spread_of_group(GROUPS[n + 1], False)
+                gate_of_group(GROUPS[n + 1])
+            body(group)
+            if n == 0:
+                grouped_1 = flip_xt(1)
+                grouped_2 = flip_xt(2)
+                packed_of[1] = quantise(grouped_1)
+                packed_of[2] = quantise(grouped_2)
+            if group[2] == FEATURE_TILES:
+                if b + 1 < BATCHES:
+                    old_share(b + 1)
+                if b + 2 < BATCHES:
+                    eps_of[b + 2] = load_batch(eps_rows, b + 2, "eps_sb")
+                    x_of[b + 2] = load_batch(x_rows, b + 2, "x_sb")
+                finish_batch(b)
+                if b == 0:
+                    packed_of[3] = quantise(flip_xt(3))
+            if n + 1 < len(GROUPS):
+                prefill(GROUPS[n + 1])

@@ -55,7 +55,7 @@ def tile_diffscm_pb_kernel(
         flip_banks = ctx.enter_context(tc.psum_pool(name="flip_banks", bufs=4))
         spread_banks = ctx.enter_context(tc.psum_pool(name="spread_banks", bufs=2))
         mean_banks = ctx.enter_context(tc.psum_pool(name="mean_banks", bufs=2))
-        ctx.enter_context(tc.manual_schedule())
+        ctx.enter_context(tc.manual_schedule(engines={mybir.EngineType.Activation}))
 
         def load_batch(source, b, label):
             rows = loads.tile([P, BATCH, FEATURES], BF16, name=label, tag=label)

@@ -52,8 +52,8 @@ def tile_diffscm_pb_kernel(
         samples = ctx.enter_context(tc.tile_pool(name="samples", bufs=3))
         gates = ctx.enter_context(tc.tile_pool(name="gates", bufs=2))
         blends = ctx.enter_context(tc.tile_pool(name="blends", bufs=2))
-        flip_banks = ctx.enter_context(tc.psum_pool(name="flip_banks", bufs=4))
-        spread_banks = ctx.enter_context(tc.psum_pool(name="spread_banks", bufs=2))
+        flip_banks = ctx.enter_context(tc.psum_pool(name="flip_banks", bufs=3))
+        spread_banks = ctx.enter_context(tc.psum_pool(name="spread_banks", bufs=3))
         mean_banks = ctx.enter_context(tc.psum_pool(name="mean_banks", bufs=2))
         ctx.enter_context(tc.manual_schedule(engines={mybir.EngineType.Activation}))
 
@@ -129,7 +129,7 @@ def tile_diffscm_pb_kernel(
             out=t_old[:], in0=t_bf[:], scalar1=-1.0, scalar2=1.0, op0=ALU.mult, op1=ALU.add
         )
 
-        def flip_xt(b):
+        def flip_xt(b, on_scalar=False):
             grouped = regroup.tile([P, PASSES * BATCH * P * PACK], BF16, align_bytes=64)
             grouped_words = grouped[:].bitcast(F32).rearrange(
                 "p (g i r u) -> p g i r u", g=PASSES, i=BATCH, u=2
@@ -144,9 +144,14 @@ def tile_diffscm_pb_kernel(
                             row_words[:, WORDS * g + u : WORDS * (g + 1) : 2],
                             identity[:],
                         )
-                nc.vector.tensor_copy(
-                    out=grouped_words[:, :, i], in_=flipped[:].rearrange("p g u r -> p g r u")
-                )
+                if on_scalar:
+                    nc.scalar.copy(
+                        out=grouped_words[:, :, i], in_=flipped[:].rearrange("p g u r -> p g r u")
+                    )
+                else:
+                    nc.vector.tensor_copy(
+                        out=grouped_words[:, :, i], in_=flipped[:].rearrange("p g u r -> p g r u")
+                    )
             return grouped
 
         def quantise(grouped):
@@ -209,7 +214,6 @@ def tile_diffscm_pb_kernel(
                 out=stretch(gate_of[b], first, end),
                 in_=stretch(sample_of[b], first, end),
                 func=ACT.Sigmoid,
-                scale=-1.0,
             )
             nc.scalar.activation(
                 out=stretch(gate_of[b], first, end),
@@ -219,15 +223,15 @@ def tile_diffscm_pb_kernel(
             )
 
         def softplus_of_group(group):
-            b, first, end = group
-            nc.vector.scalar_tensor_tensor(
-                out=stretch(sample_of[b], first, end),
-                in0=stretch(gate_of[b], first, end),
-                scalar=-1.0,
-                in1=stretch(sample_of[b], first, end),
-                op0=ALU.mult,
-                op1=ALU.max,
-            )
+            b = group[0]
+            for pair in pairs_of(group):
+                first, end = 2 * pair, 2 * pair + 2
+                nc.gpsimd.tensor_tensor(
+                    out=stretch(sample_of[b], first, end),
+                    in0=stretch(sample_of[b], first, end),
+                    in1=stretch(gate_of[b], first, end),
+                    op=ALU.subtract,
+                )
 
         def flip_eps(b, pair):
             eps_flipped = flip_banks.tile([P, 2, BATCH, P], BF16, tag="flip")
@@ -242,11 +246,13 @@ def tile_diffscm_pb_kernel(
             return eps_flipped
 
         def noise_of_pair(b, pair, eps_flipped):
-            nc.vector.tensor_tensor(
+            nc.vector.scalar_tensor_tensor(
                 out=stretch(sample_of[b], 2 * pair, 2 * pair + 2),
                 in0=stretch(sample_of[b], 2 * pair, 2 * pair + 2),
+                scalar=0.0,
                 in1=eps_flipped[:].rearrange("p s i r -> p (s i r)"),
-                op=ALU.mult,
+                op0=ALU.max,
+                op1=ALU.mult,
             )
 
         def mean_product(b, c):
@@ -300,7 +306,7 @@ def tile_diffscm_pb_kernel(
 
         def finish_batch(b):
             order = [(i, half) for i in range(BATCH) for half in range(HALVES)]
-            ahead = 4
+            ahead = 3
             flipped_of = {}
             for n in range(ahead):
                 flipped_of[order[n]] = flip_sample(b, order[n][0], order[n][1])
@@ -378,6 +384,6 @@ def tile_diffscm_pb_kernel(
                     x_of[b + 2] = load_batch(x_rows, b + 2, "x_sb")
                 finish_batch(b)
                 if b == 0:
-                    packed_of[3] = quantise(flip_xt(3))
+                    packed_of[3] = quantise(flip_xt(3, True))
             if n + 1 < len(GROUPS):
                 prefill(GROUPS[n + 1])

@@ -384,6 +384,6 @@ def tile_diffscm_pb_kernel(
                     x_of[b + 2] = load_batch(x_rows, b + 2, "x_sb")
                 finish_batch(b)
                 if b == 0:
-                    packed_of[3] = quantise(flip_xt(3, True))
+                    packed_of[3] = quantise(flip_xt(3))
             if n + 1 < len(GROUPS):
                 prefill(GROUPS[n + 1])

@@ -305,7 +305,7 @@ def tile_diffscm_pb_kernel(
             )
 
         def finish_batch(b):
-            order = [(i, half) for i in range(BATCH) for half in range(HALVES)]
+            order = [(i, half) for half in range(HALVES) for i in range(BATCH)]
             ahead = 3
             flipped_of = {}
             for n in range(ahead):
@@ -313,8 +313,10 @@ def tile_diffscm_pb_kernel(
             for n in range(len(order)):
                 i, half = order[n]
                 blend_half(b, i, half, flipped_of[order[n]])
-                if half == HALVES - 1:
-                    nc.sync.dma_start(out=out_rows[:, b * BATCH + i, :], in_=blend_of[b][:, i, :])
+                cols = slice(half * BANK, (half + 1) * BANK)
+                nc.sync.dma_start(
+                    out=out_rows[:, b * BATCH + i, cols], in_=blend_of[b][:, i, cols]
+                )
                 if n + ahead < len(order):
                     later = order[n + ahead]
                     flipped_of[later] = flip_sample(b, later[0], later[1])

@@ -238,10 +238,12 @@ def tile_diffscm_pb_kernel(
             for side in range(2):
                 c = 2 * pair + side
                 for i in range(BATCH):
-                    nc.tensor.transpose(
+                    nc.tensor.matmul(
                         eps_flipped[:, side, i, :],
-                        eps_of[b][:, i, c * P : (c + 1) * P],
-                        identity_bf[:],
+                        lhsT=eps_of[b][:, i, c * P : (c + 1) * P],
+                        rhs=identity_bf[:],
+                        start=True,
+                        stop=True,
                     )
             return eps_flipped
 

@@ -371,10 +371,11 @@ def tile_diffscm_pb_kernel(
             group = GROUPS[n]
             b = group[0]
             softplus_of_group(group)
-            if n >= 1 and n + 1 < len(GROUPS):
-                spread_of_group(GROUPS[n + 1], False)
-                gate_of_group(GROUPS[n + 1])
-            body(group)
+            with tc.high_priority():
+                if n >= 1 and n + 1 < len(GROUPS):
+                    spread_of_group(GROUPS[n + 1], False)
+                    gate_of_group(GROUPS[n + 1])
+                body(group)
             if n == 0:
                 grouped_1 = flip_xt(1)
                 grouped_2 = flip_xt(2)
@@ -390,4 +391,5 @@ def tile_diffscm_pb_kernel(
                 if b == 0:
                     packed_of[3] = quantise(flip_xt(3))
             if n + 1 < len(GROUPS):
-                prefill(GROUPS[n + 1])
+                with tc.high_priority():
+                    prefill(GROUPS[n + 1])

@@ -23,15 +23,21 @@ ROW_TILES = ROWS // P
 BATCH = 4
 BATCHES = ROW_TILES // BATCH
 BANK = 512
-HALVES = FEATURES // BANK
 FEATURE_TILES = FEATURES // P
+PAIRS = FEATURE_TILES // 2
+ALL_PAIRS = BATCHES * PAIRS
 WORDS = K_PASS // 2
 SPREAD, MEAN = 0, 1
 LN_FLOOR = 2.0**-60
 
-GROUPS = ((0, 0, 2), (0, 2, 8), (1, 0, 8), (2, 0, 8), (3, 0, 6), (3, 6, 8))
-
 FLOPS = 2 * ROWS * FEATURES * 2 * FEATURES
+
+GROUPS = (1, 3, 4, 4, 3, 1)
+V_EVAC = set(range(2, 12))
+STEP_AT = [6, 8, 10] + [2 * q + 9 for q in range(3, 16)]
+XT_AT = {4: (8, 9), 5: (10, 11), 12: (12,), 13: (13,), 14: (14,), 15: (15,)}
+Q_AT = {6: (2,), 17: (3,)}
+OLD_AT = {0: (0,), 1: (1,2), 2: (3,), 3: (4,), 12: (5,), 13: (6,), 14: (7,), **{2 * m + 2: (m,) for m in range(8, 16)}}
 
 
 def tile_diffscm_pb_kernel(
@@ -49,31 +55,31 @@ def tile_diffscm_pb_kernel(
         loads = ctx.enter_context(tc.tile_pool(name="loads", bufs=2))
         regroup = ctx.enter_context(tc.tile_pool(name="regroup", bufs=2))
         packed = ctx.enter_context(tc.tile_pool(name="packed", bufs=BATCHES))
-        samples = ctx.enter_context(tc.tile_pool(name="samples", bufs=3))
-        gates = ctx.enter_context(tc.tile_pool(name="gates", bufs=2))
-        blends = ctx.enter_context(tc.tile_pool(name="blends", bufs=2))
-        flip_banks = ctx.enter_context(tc.psum_pool(name="flip_banks", bufs=3))
+        samples = ctx.enter_context(tc.tile_pool(name="samples", bufs=12))
+        gates = ctx.enter_context(tc.tile_pool(name="gates", bufs=8))
+        blends = ctx.enter_context(tc.tile_pool(name="blends", bufs=8))
+        flip_banks = ctx.enter_context(tc.psum_pool(name="flip_banks", bufs=2))
+        eps_banks = ctx.enter_context(tc.psum_pool(name="eps_banks", bufs=1))
         spread_banks = ctx.enter_context(tc.psum_pool(name="spread_banks", bufs=3))
         mean_banks = ctx.enter_context(tc.psum_pool(name="mean_banks", bufs=2))
-        ctx.enter_context(tc.manual_schedule(engines={mybir.EngineType.Activation}))
 
         def load_batch(source, b, label):
             rows = loads.tile([P, BATCH, FEATURES], BF16, name=label, tag=label)
             nc.sync.dma_start(out=rows[:], in_=source[:, b * BATCH : (b + 1) * BATCH, :])
             return rows
 
+        xt_of = {}
+
         def load_xt_batch(b):
-            tiles = []
             for i in range(BATCH):
                 xt_sb = xt_tiles.tile([P, FEATURES], BF16)
                 nc.sync.dma_start(out=xt_sb[:], in_=xt_rows[:, b * BATCH + i, :])
-                tiles.append(xt_sb)
-            return tiles
+                xt_of[b * BATCH + i] = xt_sb
 
-        w_scales = const.tile([P, 2, PASSES, FEATURES], U8, align_bytes=64)
-        nc.vector.memset(w_scales[:].rearrange("p h g n -> p (h g n)").bitcast(I32), 0)
         identity = const.tile([P, P], F32)
         make_identity(nc, identity[:])
+        w_scales = const.tile([P, 2, PASSES, FEATURES], U8, align_bytes=64)
+        nc.vector.memset(w_scales[:].rearrange("p h g n -> p (h g n)").bitcast(I32), 0)
         identity_bf = const.tile([P, P], BF16)
         make_identity(nc, identity_bf[:])
 
@@ -92,19 +98,23 @@ def tile_diffscm_pb_kernel(
                 in_=words.bitcast(I32).rearrange("g p w -> p g w"),
             )
 
-        xt_of = {0: load_xt_batch(0)}
+        eps_of = {}
+        x_of = {}
+        load_xt_batch(0)
+        load_xt_batch(1)
         load_weights(SPREAD, Wv_words, Wv_scales)
         load_weights(MEAN, Wm_words, Wm_scales)
-        eps_of = {0: load_batch(eps_rows, 0, "eps_sb")}
-        xt_of[1] = load_xt_batch(1)
-        xt_of[2] = load_xt_batch(2)
-        x_of = {0: load_batch(x_rows, 0, "x_sb")}
-        xt_of[3] = load_xt_batch(3)
+        eps_of[0] = load_batch(eps_rows, 0, "eps_sb")
+        x_of[0] = load_batch(x_rows, 0, "x_sb")
+        load_xt_batch(2)
+        load_xt_batch(3)
         eps_of[1] = load_batch(eps_rows, 1, "eps_sb")
         x_of[1] = load_batch(x_rows, 1, "x_sb")
 
         bias_square_bf = const.tile([P, P], BF16)
         nc.vector.memset(bias_square_bf[:], 0.0)
+        warm = const.tile([P, 1], F32)
+        nc.vector.memset(warm[:], 0.0)
         nc.scalar.dma_start(
             out=bias_square_bf[0:FEATURE_TILES, :], in_=bv.rearrange("(c n) -> c n", n=P)
         )
@@ -114,60 +124,54 @@ def tile_diffscm_pb_kernel(
         )
         t_bf = const.tile([P, ROW_TILES], BF16)
         nc.scalar.dma_start(out=t_bf[:], in_=t_rand.rearrange("(p i) o -> p (i o)", i=ROW_TILES))
-        warm = const.tile([P, 1], F32)
-        nc.vector.memset(warm[:], 0.0)
         nc.scalar.activation(out=warm[:], in_=warm[:], func=ACT.Sigmoid)
 
-        bias_square = const.tile([P, P], F32)
-        nc.vector.tensor_copy(out=bias_square[:], in_=bias_square_bf[:])
-        bias_col = const.tile([P, 2 * FEATURE_TILES], F32)
+        grouped_of = {}
+        xt_flipped_of = {}
+        packed_of = {}
 
-        t_new = const.tile([P, ROW_TILES], F32)
-        nc.vector.tensor_copy(out=t_new[:], in_=t_bf[:])
-        t_old = const.tile([P, ROW_TILES], F32)
-        nc.vector.tensor_scalar(
-            out=t_old[:], in0=t_bf[:], scalar1=-1.0, scalar2=1.0, op0=ALU.mult, op1=ALU.add
-        )
+        def flip_xt(m):
+            row_words = xt_of[m][:].bitcast(F32)
+            if m < 8 and m % 4 >= 2:
+                flipped = mean_banks.tile([P, PASSES, 2, P], F32, tag="mean")
+            else:
+                flipped = flip_banks.tile([P, PASSES, 2, P], F32, tag="flip")
+            for g in range(PASSES):
+                for u in range(2):
+                    nc.tensor.transpose(
+                        flipped[:, g, u, :],
+                        row_words[:, WORDS * g + u : WORDS * (g + 1) : 2],
+                        identity[:],
+                    )
+            xt_flipped_of[m] = flipped
 
-        def flip_xt(b, on_scalar=False):
-            grouped = regroup.tile([P, PASSES * BATCH * P * PACK], BF16, align_bytes=64)
-            grouped_words = grouped[:].bitcast(F32).rearrange(
+        def copy_xt(m, on_scalar=False):
+            b, i = m // BATCH, m % BATCH
+            if i == 0:
+                grouped = regroup.tile([P, PASSES * BATCH * P * PACK], BF16, align_bytes=64)
+                grouped_of[b] = grouped
+            words = grouped_of[b][:].bitcast(F32).rearrange(
                 "p (g i r u) -> p g i r u", g=PASSES, i=BATCH, u=2
             )
-            for i in range(BATCH):
-                row_words = xt_of[b][i][:].bitcast(F32)
-                flipped = flip_banks.tile([P, PASSES, 2, P], F32, tag="flip")
-                for g in range(PASSES):
-                    for u in range(2):
-                        nc.tensor.transpose(
-                            flipped[:, g, u, :],
-                            row_words[:, WORDS * g + u : WORDS * (g + 1) : 2],
-                            identity[:],
-                        )
-                if on_scalar:
-                    nc.scalar.copy(
-                        out=grouped_words[:, :, i], in_=flipped[:].rearrange("p g u r -> p g r u")
-                    )
-                else:
-                    nc.vector.tensor_copy(
-                        out=grouped_words[:, :, i], in_=flipped[:].rearrange("p g u r -> p g r u")
-                    )
-            return grouped
+            source = xt_flipped_of[m][:].rearrange("p g u r -> p g r u")
+            if on_scalar:
+                nc.scalar.copy(out=words[:, :, i], in_=source)
+            else:
+                nc.vector.tensor_copy(out=words[:, :, i], in_=source)
 
-        def quantise(grouped):
+        def quantise(b):
             codes = packed.tile([P, PASSES, BATCH, P], U32, align_bytes=64)
             code_scales = packed.tile([P, PASSES, BATCH, P], U8, align_bytes=64)
-            nc.vector.quantize_mx(
-                out=codes[:].rearrange("p g i r -> p (g i r)").bitcast(FP8X4),
-                scales=code_scales[:].rearrange("p g i r -> p (g i r)"),
-                in_=grouped[:],
-            )
-            return codes, code_scales
-
-        packed_of = {}
-        sample_of = {}
-        gate_of = {}
-        blend_of = {}
+            half = PASSES * BATCH * P // 2
+            flat_codes = codes[:].rearrange("p g i r -> p (g i r)")
+            flat_scales = code_scales[:].rearrange("p g i r -> p (g i r)")
+            for g in range(PASSES):
+                nc.vector.quantize_mx(
+                    out=flat_codes[:, g * half : (g + 1) * half].bitcast(FP8X4),
+                    scales=flat_scales[:, g * half : (g + 1) * half],
+                    in_=grouped_of[b][:, g * half * PACK : (g + 1) * half * PACK],
+                )
+            packed_of[b] = (codes, code_scales)
 
         def product(bank, head, b, c):
             codes, code_scales = packed_of[b]
@@ -182,59 +186,58 @@ def tile_diffscm_pb_kernel(
                     stop=(g == PASSES - 1),
                 )
 
-        def spread_of_group(group, on_vector):
-            b, first, end = group
-            if b not in sample_of:
-                sample = samples.tile([P, FEATURE_TILES, BATCH * P], F32)
-                sample_of[b] = sample
-            for c in range(first, end):
-                sums = spread_banks.tile([P, BANK], F32, tag="spread")
-                product(sums, SPREAD, b, c)
-                if on_vector:
-                    nc.vector.tensor_scalar_add(
-                        out=sample_of[b][:, c, :], in0=sums[:], scalar1=bias_col[:, c : c + 1]
-                    )
-                else:
-                    nc.scalar.activation(
-                        out=sample_of[b][:, c, :],
-                        in_=sums[:],
-                        func=ACT.Identity,
-                        bias=bias_col[:, c : c + 1],
-                    )
+        sample_of = {}
+        gate_of = {}
+        spread_of = {}
+        mean_of = {}
+        eps_flipped_of = {}
+        sample_flipped_of = {}
+        blend_of = {}
 
-        def stretch(tile_, first, end):
-            return tile_[:, first:end, :].rearrange("p c b -> p (c b)")
+        def flat(tile_):
+            return tile_[:].rearrange("p s b -> p (s b)")
 
-        def gate_of_group(group):
-            b, first, end = group
-            if b not in gate_of:
-                log_gate = gates.tile([P, FEATURE_TILES, BATCH * P], F32)
-                gate_of[b] = log_gate
-            nc.scalar.activation(
-                out=stretch(gate_of[b], first, end),
-                in_=stretch(sample_of[b], first, end),
-                func=ACT.Sigmoid,
-            )
-            nc.scalar.activation(
-                out=stretch(gate_of[b], first, end),
-                in_=stretch(gate_of[b], first, end),
-                func=ACT.Ln,
-                bias=LN_FLOOR,
-            )
+        def spread_product(j):
+            sums = spread_banks.tile([P, BANK], F32, tag="spread")
+            product(sums, SPREAD, j // FEATURE_TILES, j % FEATURE_TILES)
+            spread_of[j] = sums
 
-        def softplus_of_group(group):
-            b = group[0]
-            for pair in pairs_of(group):
-                first, end = 2 * pair, 2 * pair + 2
-                nc.gpsimd.tensor_tensor(
-                    out=stretch(sample_of[b], first, end),
-                    in0=stretch(sample_of[b], first, end),
-                    in1=stretch(gate_of[b], first, end),
-                    op=ALU.subtract,
+        def evacuate(j):
+            q, side, c = j // 2, j % 2, j % FEATURE_TILES
+            if side == 0:
+                sample = samples.tile([P, 2, BANK], F32)
+                sample_of[q] = sample
+            if j in V_EVAC:
+                nc.vector.tensor_scalar_add(
+                    out=sample_of[q][:, side, :], in0=spread_of[j][:], scalar1=bias_col[:, c : c + 1]
+                )
+            else:
+                nc.scalar.activation(
+                    out=sample_of[q][:, side, :],
+                    in_=spread_of[j][:],
+                    func=ACT.Identity,
+                    bias=bias_col[:, c : c + 1],
                 )
 
-        def flip_eps(b, pair):
-            eps_flipped = flip_banks.tile([P, 2, BATCH, P], BF16, tag="flip")
+        def sigmoid(q):
+            gate = gates.tile([P, 2, BANK], F32)
+            gate_of[q] = gate
+            nc.scalar.activation(out=flat(gate), in_=flat(sample_of[q]), func=ACT.Sigmoid)
+
+        def logarithm(q):
+            nc.scalar.activation(
+                out=flat(gate_of[q]), in_=flat(gate_of[q]), func=ACT.Ln, bias=LN_FLOOR
+            )
+
+        def subtract(q, on_vector=False):
+            engine = nc.vector if on_vector else nc.gpsimd
+            engine.tensor_tensor(
+                out=flat(sample_of[q]), in0=flat(sample_of[q]), in1=flat(gate_of[q]), op=ALU.subtract
+            )
+
+        def flip_eps(q):
+            b, pair = q // PAIRS, q % PAIRS
+            eps_flipped = eps_banks.tile([P, 2, BATCH, P], BF16, tag="eps")
             for side in range(2):
                 c = 2 * pair + side
                 for i in range(BATCH):
@@ -245,151 +248,207 @@ def tile_diffscm_pb_kernel(
                         start=True,
                         stop=True,
                     )
-            return eps_flipped
+            eps_flipped_of[q] = eps_flipped
 
-        def noise_of_pair(b, pair, eps_flipped):
+        def noise(q):
             nc.vector.scalar_tensor_tensor(
-                out=stretch(sample_of[b], 2 * pair, 2 * pair + 2),
-                in0=stretch(sample_of[b], 2 * pair, 2 * pair + 2),
+                out=flat(sample_of[q]),
+                in0=flat(sample_of[q]),
                 scalar=0.0,
-                in1=eps_flipped[:].rearrange("p s i r -> p (s i r)"),
+                in1=eps_flipped_of[q][:].rearrange("p s i r -> p (s i r)"),
                 op0=ALU.max,
                 op1=ALU.mult,
             )
 
-        def mean_product(b, c):
+        def mean_product(q, side):
             sums = mean_banks.tile([P, BANK], F32, tag="mean")
-            product(sums, MEAN, b, c)
-            return sums
+            product(sums, MEAN, q // PAIRS, 2 * (q % PAIRS) + side)
+            mean_of[(q, side)] = sums
 
-        def sample_of_tile(b, c, sums):
+        def add_mean(q, side):
+            c = FEATURE_TILES + 2 * (q % PAIRS) + side
             nc.vector.scalar_tensor_tensor(
-                out=sample_of[b][:, c, :],
-                in0=sums[:],
-                scalar=bias_col[:, FEATURE_TILES + c : FEATURE_TILES + c + 1],
-                in1=sample_of[b][:, c, :],
+                out=sample_of[q][:, side, :],
+                in0=mean_of[(q, side)][:],
+                scalar=bias_col[:, c : c + 1],
+                in1=sample_of[q][:, side, :],
                 op0=ALU.add,
                 op1=ALU.add,
             )
 
-        def old_share(b):
-            blend = blends.tile([P, BATCH, FEATURES], F32)
-            blend_of[b] = blend
-            for i in range(BATCH):
-                nc.gpsimd.tensor_scalar(
-                    out=blend[:, i, :],
-                    in0=x_of[b][:, i, :],
-                    scalar1=t_old[:, b * BATCH + i : b * BATCH + i + 1],
-                    scalar2=0.0,
-                    op0=ALU.mult,
-                    op1=ALU.add,
-                )
-
-        def flip_sample(b, i, half):
-            flipped = flip_banks.tile([P, BANK // P, P], F32, tag="flip")
-            for q in range(BANK // P):
-                nc.tensor.transpose(
-                    flipped[:, q, :],
-                    sample_of[b][:, half * (BANK // P) + q, i * P : (i + 1) * P],
-                    identity[:],
-                )
-            return flipped
-
-        def blend_half(b, i, half, flipped):
-            cols = slice(half * BANK, (half + 1) * BANK)
-            nc.vector.scalar_tensor_tensor(
-                out=blend_of[b][:, i, cols],
-                in0=flipped[:].rearrange("p q n -> p (q n)"),
-                scalar=t_new[:, b * BATCH + i : b * BATCH + i + 1],
-                in1=blend_of[b][:, i, cols],
+        def old_share(m):
+            blend = blends.tile([P, FEATURES], F32)
+            blend_of[m] = blend
+            nc.gpsimd.tensor_scalar(
+                out=blend[:],
+                in0=x_of[m // BATCH][:, m % BATCH, :],
+                scalar1=t_old[:, m : m + 1],
+                scalar2=0.0,
                 op0=ALU.mult,
                 op1=ALU.add,
             )
 
-        def finish_batch(b):
-            order = [(i, half) for half in range(HALVES) for i in range(BATCH)]
-            ahead = 3
-            flipped_of = {}
-            for n in range(ahead):
-                flipped_of[order[n]] = flip_sample(b, order[n][0], order[n][1])
-            for n in range(len(order)):
-                i, half = order[n]
-                blend_half(b, i, half, flipped_of[order[n]])
-                cols = slice(half * BANK, (half + 1) * BANK)
-                nc.sync.dma_start(
-                    out=out_rows[:, b * BATCH + i, cols], in_=blend_of[b][:, i, cols]
+        def split(n):
+            return n // 8, (n % 8) // BATCH, n % BATCH
+
+        def flip_sample(n):
+            b, half, i = split(n)
+            flipped = flip_banks.tile([P, BANK // P, P], F32, tag="flip")
+            for k in range(BANK // P):
+                sample = sample_of[b * PAIRS + 2 * half + k // 2]
+                nc.tensor.transpose(
+                    flipped[:, k, :], sample[:, k % 2, i * P : (i + 1) * P], identity[:]
                 )
-                if n + ahead < len(order):
-                    later = order[n + ahead]
-                    flipped_of[later] = flip_sample(b, later[0], later[1])
+            sample_flipped_of[n] = flipped
 
-        eps_ready = {}
-        mean_ready = {}
+        def blend(n):
+            b, half, i = split(n)
+            m = b * BATCH + i
+            cols = slice(half * BANK, (half + 1) * BANK)
+            nc.vector.scalar_tensor_tensor(
+                out=blend_of[m][:, cols],
+                in0=sample_flipped_of[n][:].rearrange("p k n -> p (k n)"),
+                scalar=t_new[:, m : m + 1],
+                in1=blend_of[m][:, cols],
+                op0=ALU.mult,
+                op1=ALU.add,
+            )
+            nc.sync.dma_start(out=out_rows[:, m, cols], in_=blend_of[m][:, cols])
 
-        def pairs_of(group):
-            return list(range(group[1] // 2, group[2] // 2))
+        items = []
+        first = 0
+        for size in GROUPS:
+            items += [(0, q) for q in range(first, first + size)]
+            items += [(1, q) for q in range(first, first + size)]
+            first += size
+        emptied = 2
+        before = []
+        early = [[] for n in range(len(items))]
+        for n in range(len(items)):
+            kind, q = items[n]
+            need = 2 * (q + 1) if kind == 0 else 0
+            count = max(need - emptied, 1 if n >= 5 else 0)
+            count = min(count, 2 * ALL_PAIRS - emptied)
+            before.append([j for j in range(emptied, emptied + count) if j not in V_EVAC])
+            for j in range(emptied, emptied + count):
+                if j in V_EVAC:
+                    early[max(n - 0, 0)].append(j)
+            emptied += count
+        sequence = [j for n in range(len(items)) for j in early[n] + before[n]]
 
-        def prefill(group):
-            b = group[0]
-            pairs = pairs_of(group)
-            for pair in pairs[0:2]:
-                eps_ready[(b, pair)] = flip_eps(b, pair)
-            for side in range(2):
-                c = 2 * pairs[0] + side
-                mean_ready[(b, c)] = mean_product(b, c)
+        every = {
+            mybir.EngineType.PE,
+            mybir.EngineType.Activation,
+            mybir.EngineType.DVE,
+            mybir.EngineType.Pool,
+        }
+        with tc.manual_schedule(engines=every):
+            for i in range(BATCH):
+                flip_xt(i)
+                copy_xt(i, i % 2 == 1)
+            bias_square = const.tile([P, P], F32)
+            nc.vector.tensor_copy(out=bias_square[:], in_=bias_square_bf[:])
+            bias_flipped = eps_banks.tile([P, P], F32, tag="eps")
+            nc.tensor.transpose(bias_flipped[:], bias_square[:], identity[:])
+            bias_col = const.tile([P, 2 * FEATURE_TILES], F32)
+            nc.vector.tensor_copy(out=bias_col[:], in_=bias_flipped[:, 0 : 2 * FEATURE_TILES])
+            quantise(0)
+            for i in range(BATCH):
+                flip_xt(BATCH + i)
+                copy_xt(BATCH + i, i < 4)
+            t_new = const.tile([P, ROW_TILES], F32)
+            nc.vector.tensor_copy(out=t_new[:], in_=t_bf[:])
+            t_old = const.tile([P, ROW_TILES], F32)
+            nc.vector.tensor_scalar(
+                out=t_old[:], in0=t_bf[:], scalar1=-1.0, scalar2=1.0, op0=ALU.mult, op1=ALU.add
+            )
+            spread_product(0)
+            spread_product(1)
+            evacuate(0)
+            evacuate(1)
+            quantise(1)
+        state = {"flips": 0, "blends": 0, "product": 0, "empty": 0}
 
-        def body(group):
-            b = group[0]
-            pairs = pairs_of(group)
-            noise_of_pair(b, pairs[0], eps_ready[(b, pairs[0])])
-            for j in range(len(pairs)):
-                pair = pairs[j]
-                if j + 2 < len(pairs):
-                    eps_ready[(b, pairs[j + 2])] = flip_eps(b, pairs[j + 2])
-                if j + 1 < len(pairs):
-                    noise_of_pair(b, pairs[j + 1], eps_ready[(b, pairs[j + 1])])
-                for side in range(2):
-                    c = 2 * pair + side
-                    sample_of_tile(b, c, mean_ready[(b, c)])
-                    if j + 1 < len(pairs):
-                        later = 2 * pairs[j + 1] + side
-                        mean_ready[(b, later)] = mean_product(b, later)
+        def products(count):
+            while state["product"] < min(count, len(sequence)):
+                spread_product(sequence[state["product"]])
+                state["product"] += 1
 
-        packed_of[0] = quantise(flip_xt(0))
-        bias_flipped = flip_banks.tile([P, P], F32, tag="flip")
-        nc.tensor.transpose(bias_flipped[:], bias_square[:], identity[:])
-        nc.vector.tensor_copy(out=bias_col[:], in_=bias_flipped[:, 0 : 2 * FEATURE_TILES])
+        def blend_next():
+            if state["blends"] < state["flips"]:
+                blend(state["blends"])
+                state["blends"] += 1
 
-        spread_of_group(GROUPS[0], False)
-        gate_of_group(GROUPS[0])
-        spread_of_group(GROUPS[1], True)
-        gate_of_group(GROUPS[1])
-        old_share(0)
-        prefill(GROUPS[0])
+        def flip_next(limit):
+            if state["flips"] < limit:
+                flip_sample(state["flips"])
+                state["flips"] += 1
 
-        for n in range(len(GROUPS)):
-            group = GROUPS[n]
-            b = group[0]
-            softplus_of_group(group)
-            with tc.high_priority():
-                if n >= 1 and n + 1 < len(GROUPS):
-                    spread_of_group(GROUPS[n + 1], False)
-                    gate_of_group(GROUPS[n + 1])
-                body(group)
-            if n == 0:
-                grouped_1 = flip_xt(1)
-                grouped_2 = flip_xt(2)
-                packed_of[1] = quantise(grouped_1)
-                packed_of[2] = quantise(grouped_2)
-            if group[2] == FEATURE_TILES:
-                if b + 1 < BATCHES:
-                    old_share(b + 1)
-                if b + 2 < BATCHES:
-                    eps_of[b + 2] = load_batch(eps_rows, b + 2, "eps_sb")
-                    x_of[b + 2] = load_batch(x_rows, b + 2, "x_sb")
-                finish_batch(b)
-                if b == 0:
-                    packed_of[3] = quantise(flip_xt(3))
-            if n + 1 < len(GROUPS):
-                with tc.high_priority():
-                    prefill(GROUPS[n + 1])
+        def step_half(q, half):
+            if half == 0:
+                mean_product(q, 1)
+                for k in range(2):
+                    flip_next(4 * (q // 2))
+                if q + 1 < ALL_PAIRS:
+                    noise(q + 1)
+                add_mean(q, 0)
+                blend_next()
+            else:
+                if q + 2 < ALL_PAIRS:
+                    flip_eps(q + 2)
+                if q + 1 < ALL_PAIRS:
+                    mean_product(q + 1, 0)
+                add_mean(q, 1)
+                blend_next()
+
+        def prologue():
+            flip_eps(0)
+            noise(0)
+            mean_product(0, 0)
+            flip_eps(1)
+
+        def work(slot):
+            for m in XT_AT.get(slot, ()):
+                flip_xt(m)
+            for m in XT_AT.get(slot - 1, ()):
+                copy_xt(m)
+            for b in Q_AT.get(slot, ()):
+                quantise(b)
+            for m in OLD_AT.get(slot, ()):
+                if m % BATCH == 0 and m // BATCH >= 2:
+                    x_of[m // BATCH] = load_batch(x_rows, m // BATCH, "x_sb")
+                old_share(m)
+
+        with tc.manual_schedule(engines={mybir.EngineType.Activation}):
+            step_of = {}
+            for q in range(ALL_PAIRS):
+                step_of.setdefault(STEP_AT[q], []).append((q, 0))
+                step_of.setdefault(STEP_AT[q] + 1, []).append((q, 1))
+            last_slot = max(list(step_of) + [len(items)])
+            for n in range(last_slot + 1):
+                if n < len(items):
+                    now = early[n] + before[n]
+                    products(state["empty"] + len(now))
+                    state["empty"] += len(now)
+                    if n + 1 < len(items):
+                        products(state["empty"] + min(len(early[n + 1] + before[n + 1]), 2))
+                    for j in now:
+                        evacuate(j)
+                    kind, q = items[n]
+                    if kind == 0:
+                        sigmoid(q)
+                    else:
+                        logarithm(q)
+                        subtract(q, q == 0 and False)
+                work(n)
+                if n == 4:
+                    prologue()
+                for q, half in step_of.get(n, ()):
+                    if half == 0 and q % PAIRS == 0 and q // PAIRS + 2 < BATCHES and q // PAIRS >= 0:
+                        eps_of[q // PAIRS + 2] = load_batch(eps_rows, q // PAIRS + 2, "eps_sb")
+                    step_half(q, half)
+            while state["blends"] < 32:
+                flip_next(32)
+                flip_next(32)
+                blend_next()
+                blend_next()

@@ -33,11 +33,6 @@ LN_FLOOR = 2.0**-60
 FLOPS = 2 * ROWS * FEATURES * 2 * FEATURES
 
 GROUPS = (1, 3, 4, 4, 3, 1)
-V_EVAC = set(range(2, 12))
-STEP_AT = [6, 8, 10] + [2 * q + 9 for q in range(3, 16)]
-XT_AT = {4: (8, 9), 5: (10, 11), 12: (12,), 13: (13,), 14: (14,), 15: (15,)}
-Q_AT = {6: (2,), 17: (3,)}
-OLD_AT = {0: (0,), 1: (1,2), 2: (3,), 3: (4,), 12: (5,), 13: (6,), 14: (7,), **{2 * m + 2: (m,) for m in range(8, 16)}}
 
 
 def tile_diffscm_pb_kernel(
@@ -58,6 +53,7 @@ def tile_diffscm_pb_kernel(
         samples = ctx.enter_context(tc.tile_pool(name="samples", bufs=12))
         gates = ctx.enter_context(tc.tile_pool(name="gates", bufs=8))
         blends = ctx.enter_context(tc.tile_pool(name="blends", bufs=8))
+        weights = ctx.enter_context(tc.tile_pool(name="weights", bufs=3))
         flip_banks = ctx.enter_context(tc.psum_pool(name="flip_banks", bufs=2))
         eps_banks = ctx.enter_context(tc.psum_pool(name="eps_banks", bufs=1))
         spread_banks = ctx.enter_context(tc.psum_pool(name="spread_banks", bufs=3))
@@ -105,9 +101,9 @@ def tile_diffscm_pb_kernel(
         load_weights(SPREAD, Wv_words, Wv_scales)
         load_weights(MEAN, Wm_words, Wm_scales)
         eps_of[0] = load_batch(eps_rows, 0, "eps_sb")
-        x_of[0] = load_batch(x_rows, 0, "x_sb")
         load_xt_batch(2)
         load_xt_batch(3)
+        x_of[0] = load_batch(x_rows, 0, "x_sb")
         eps_of[1] = load_batch(eps_rows, 1, "eps_sb")
         x_of[1] = load_batch(x_rows, 1, "x_sb")
 
@@ -132,7 +128,7 @@ def tile_diffscm_pb_kernel(
 
         def flip_xt(m):
             row_words = xt_of[m][:].bitcast(F32)
-            if m < 8 and m % 4 >= 2:
+            if m % 4 >= 2:
                 flipped = mean_banks.tile([P, PASSES, 2, P], F32, tag="mean")
             else:
                 flipped = flip_banks.tile([P, PASSES, 2, P], F32, tag="flip")
@@ -202,12 +198,12 @@ def tile_diffscm_pb_kernel(
             product(sums, SPREAD, j // FEATURE_TILES, j % FEATURE_TILES)
             spread_of[j] = sums
 
-        def evacuate(j):
+        def evacuate(j, by_vector=False):
             q, side, c = j // 2, j % 2, j % FEATURE_TILES
             if side == 0:
                 sample = samples.tile([P, 2, BANK], F32)
                 sample_of[q] = sample
-            if j in V_EVAC:
+            if by_vector:
                 nc.vector.tensor_scalar_add(
                     out=sample_of[q][:, side, :], in0=spread_of[j][:], scalar1=bias_col[:, c : c + 1]
                 )
@@ -301,10 +297,23 @@ def tile_diffscm_pb_kernel(
                 )
             sample_flipped_of[n] = flipped
 
-        def blend(n):
+        def blend(n, split_blend=False):
             b, half, i = split(n)
             m = b * BATCH + i
             cols = slice(half * BANK, (half + 1) * BANK)
+            if split_blend:
+                weighed = weights.tile([P, BANK], F32)
+                nc.scalar.activation(
+                    out=weighed[:],
+                    in_=sample_flipped_of[n][:].rearrange("p k n -> p (k n)"),
+                    func=ACT.Copy,
+                    scale=t_new[:, m : m + 1],
+                )
+                nc.gpsimd.tensor_tensor(
+                    out=blend_of[m][:, cols], in0=weighed[:], in1=blend_of[m][:, cols], op=ALU.add
+                )
+                nc.sync.dma_start(out=out_rows[:, m, cols], in_=blend_of[m][:, cols])
+                return
             nc.vector.scalar_tensor_tensor(
                 out=blend_of[m][:, cols],
                 in0=sample_flipped_of[n][:].rearrange("p k n -> p (k n)"),
@@ -315,74 +324,58 @@ def tile_diffscm_pb_kernel(
             )
             nc.sync.dma_start(out=out_rows[:, m, cols], in_=blend_of[m][:, cols])
 
+
         items = []
         first = 0
         for size in GROUPS:
             items += [(0, q) for q in range(first, first + size)]
             items += [(1, q) for q in range(first, first + size)]
             first += size
-        emptied = 2
         before = []
-        early = [[] for n in range(len(items))]
+        emptied = 16
         for n in range(len(items)):
             kind, q = items[n]
             need = 2 * (q + 1) if kind == 0 else 0
-            count = max(need - emptied, 1 if n >= 5 else 0)
-            count = min(count, 2 * ALL_PAIRS - emptied)
-            before.append([j for j in range(emptied, emptied + count) if j not in V_EVAC])
-            for j in range(emptied, emptied + count):
-                if j in V_EVAC:
-                    early[max(n - 0, 0)].append(j)
+            count = max(need - emptied, 1 if n >= 12 else 0)
+            count = max(min(count, 2 * ALL_PAIRS - emptied), 0)
+            before.append(list(range(emptied, emptied + count)))
             emptied += count
-        sequence = [j for n in range(len(items)) for j in early[n] + before[n]]
 
-        every = {
-            mybir.EngineType.PE,
-            mybir.EngineType.Activation,
-            mybir.EngineType.DVE,
-            mybir.EngineType.Pool,
-        }
-        with tc.manual_schedule(engines=every):
-            for i in range(BATCH):
-                flip_xt(i)
-                copy_xt(i, i % 2 == 1)
-            bias_square = const.tile([P, P], F32)
-            nc.vector.tensor_copy(out=bias_square[:], in_=bias_square_bf[:])
-            bias_flipped = eps_banks.tile([P, P], F32, tag="eps")
-            nc.tensor.transpose(bias_flipped[:], bias_square[:], identity[:])
-            bias_col = const.tile([P, 2 * FEATURE_TILES], F32)
-            nc.vector.tensor_copy(out=bias_col[:], in_=bias_flipped[:, 0 : 2 * FEATURE_TILES])
-            quantise(0)
-            for i in range(BATCH):
-                flip_xt(BATCH + i)
-                copy_xt(BATCH + i, i < 4)
-            t_new = const.tile([P, ROW_TILES], F32)
-            nc.vector.tensor_copy(out=t_new[:], in_=t_bf[:])
-            t_old = const.tile([P, ROW_TILES], F32)
-            nc.vector.tensor_scalar(
-                out=t_old[:], in0=t_bf[:], scalar1=-1.0, scalar2=1.0, op0=ALU.mult, op1=ALU.add
-            )
-            spread_product(0)
-            spread_product(1)
-            evacuate(0)
-            evacuate(1)
-            quantise(1)
-        state = {"flips": 0, "blends": 0, "product": 0, "empty": 0}
+        state = {"flips": 0, "blends": 0, "product": 0}
 
         def products(count):
-            while state["product"] < min(count, len(sequence)):
-                spread_product(sequence[state["product"]])
+            while state["product"] < min(count, 2 * ALL_PAIRS):
+                spread_product(state["product"])
                 state["product"] += 1
 
         def blend_next():
-            if state["blends"] < state["flips"]:
-                blend(state["blends"])
+            n = state["blends"]
+            if n < state["flips"]:
+                blend(n, n >= 22 and n % 2 == 0 and n < 30)
                 state["blends"] += 1
 
         def flip_next(limit):
             if state["flips"] < limit:
                 flip_sample(state["flips"])
                 state["flips"] += 1
+
+        def function(n):
+            kind, q = items[n]
+            if kind == 0:
+                sigmoid(q)
+            else:
+                logarithm(q)
+                subtract(q)
+
+        def vector_empties(first, last):
+            for j in range(first, last):
+                products(j + 1)
+                evacuate(j, True)
+
+        def turn_xt(b, on_scalar=()):
+            for i in range(BATCH):
+                flip_xt(BATCH * b + i)
+                copy_xt(BATCH * b + i, i in on_scalar)
 
         def step_half(q, half):
             if half == 0:
@@ -401,54 +394,74 @@ def tile_diffscm_pb_kernel(
                 add_mean(q, 1)
                 blend_next()
 
-        def prologue():
+        t_new = const.tile([P, ROW_TILES], F32)
+        t_old = const.tile([P, ROW_TILES], F32)
+        bias_square = const.tile([P, P], F32)
+        bias_col = const.tile([P, 2 * FEATURE_TILES], F32)
+        every = {
+            mybir.EngineType.PE,
+            mybir.EngineType.Activation,
+            mybir.EngineType.DVE,
+            mybir.EngineType.Pool,
+        }
+        with tc.manual_schedule(engines=every):
+            turn_xt(0, (1, 3))
+            nc.vector.tensor_copy(out=bias_square[:], in_=bias_square_bf[:])
+            bias_flipped = eps_banks.tile([P, P], F32, tag="eps")
+            nc.tensor.transpose(bias_flipped[:], bias_square[:], identity[:])
+            nc.vector.tensor_copy(out=bias_col[:], in_=bias_flipped[:, 0 : 2 * FEATURE_TILES])
+            quantise(0)
+            nc.vector.tensor_copy(out=t_new[:], in_=t_bf[:])
+            nc.vector.tensor_scalar(
+                out=t_old[:], in0=t_bf[:], scalar1=-1.0, scalar2=1.0, op0=ALU.mult, op1=ALU.add
+            )
+            turn_xt(1, (0, 1, 2, 3))
+            products(2)
+            evacuate(0)
+            evacuate(1)
+            quantise(1)
+            function(0)
+            function(1)
+            vector_empties(2, 8)
+            old_share(0)
+            old_share(1)
+            old_share(2)
+            turn_xt(2)
+            for n in range(2, 5):
+                function(n)
             flip_eps(0)
             noise(0)
             mean_product(0, 0)
+            quantise(2)
+            vector_empties(8, 12)
+            turn_xt(3)
             flip_eps(1)
-
-        def work(slot):
-            for m in XT_AT.get(slot, ()):
-                flip_xt(m)
-            for m in XT_AT.get(slot - 1, ()):
-                copy_xt(m)
-            for b in Q_AT.get(slot, ()):
-                quantise(b)
-            for m in OLD_AT.get(slot, ()):
-                if m % BATCH == 0 and m // BATCH >= 2:
-                    x_of[m // BATCH] = load_batch(x_rows, m // BATCH, "x_sb")
-                old_share(m)
-
-        with tc.manual_schedule(engines={mybir.EngineType.Activation}):
-            step_of = {}
-            for q in range(ALL_PAIRS):
-                step_of.setdefault(STEP_AT[q], []).append((q, 0))
-                step_of.setdefault(STEP_AT[q] + 1, []).append((q, 1))
-            last_slot = max(list(step_of) + [len(items)])
-            for n in range(last_slot + 1):
+            for n in range(5, 8):
+                function(n)
+            quantise(3)
+            vector_empties(12, 16)
+            products(19)
+            for n in range(8, max(len(items), 2 * ALL_PAIRS + 8)):
                 if n < len(items):
-                    now = early[n] + before[n]
-                    products(state["empty"] + len(now))
-                    state["empty"] += len(now)
-                    if n + 1 < len(items):
-                        products(state["empty"] + min(len(early[n + 1] + before[n + 1]), 2))
-                    for j in now:
+                    for j in before[n]:
+                        products(j + 1)
                         evacuate(j)
-                    kind, q = items[n]
-                    if kind == 0:
-                        sigmoid(q)
-                    else:
-                        logarithm(q)
-                        subtract(q, q == 0 and False)
-                work(n)
-                if n == 4:
-                    prologue()
-                for q, half in step_of.get(n, ()):
-                    if half == 0 and q % PAIRS == 0 and q // PAIRS + 2 < BATCHES and q // PAIRS >= 0:
+                    ahead = (before[n] or before[min(n + 1, len(items) - 1)])
+                    if ahead:
+                        products(ahead[-1] + 1 + 2)
+                    function(n)
+                for m in range(ROW_TILES):
+                    if n == (9 if m == 3 else 2 * m + (4 if m < 8 else 6)):
+                        if m % BATCH == 0 and m // BATCH >= 2:
+                            x_of[m // BATCH] = load_batch(x_rows, m // BATCH, "x_sb")
+                        old_share(m)
+                q, half = (n - 8) // 2, (n - 8) % 2
+                if 0 <= q < ALL_PAIRS:
+                    if half == 0 and q % PAIRS == 0 and q // PAIRS + 2 < BATCHES:
                         eps_of[q // PAIRS + 2] = load_batch(eps_rows, q // PAIRS + 2, "eps_sb")
                     step_half(q, half)
-            while state["blends"] < 32:
-                flip_next(32)
-                flip_next(32)
+            while state["blends"] < 2 * ROW_TILES:
+                flip_next(2 * ROW_TILES)
+                flip_next(2 * ROW_TILES)
                 blend_next()
                 blend_next()

@@ -445,7 +445,7 @@ def tile_diffscm_pb_kernel(
                 if n < len(items):
                     for j in before[n]:
                         products(j + 1)
-                        evacuate(j)
+                        evacuate(j, j % 4 == 0)
                     ahead = (before[n] or before[min(n + 1, len(items) - 1)])
                     if ahead:
                         products(ahead[-1] + 1 + 2)

@@ -289,7 +289,12 @@ def tile_diffscm_pb_kernel(
 
         def flip_sample(n):
             b, half, i = split(n)
-            flipped = flip_banks.tile([P, BANK // P, P], F32, tag="flip")
+            if n < 2 * ROW_TILES - BATCH:
+                flipped = flip_banks.tile([P, BANK // P, P], F32, tag="flip")
+            elif i < 3:
+                flipped = spread_banks.tile([P, BANK // P, P], F32, tag="spread")
+            else:
+                flipped = mean_banks.tile([P, BANK // P, P], F32, tag="mean")
             for k in range(BANK // P):
                 sample = sample_of[b * PAIRS + 2 * half + k // 2]
                 nc.tensor.transpose(
@@ -385,14 +390,16 @@ def tile_diffscm_pb_kernel(
                 if q + 1 < ALL_PAIRS:
                     noise(q + 1)
                 add_mean(q, 0)
-                blend_next()
+                if q + 1 < ALL_PAIRS:
+                    blend_next()
             else:
                 if q + 2 < ALL_PAIRS:
                     flip_eps(q + 2)
                 if q + 1 < ALL_PAIRS:
                     mean_product(q + 1, 0)
                 add_mean(q, 1)
-                blend_next()
+                if q + 1 < ALL_PAIRS:
+                    blend_next()
 
         t_new = const.tile([P, ROW_TILES], F32)
         t_old = const.tile([P, ROW_TILES], F32)
@@ -426,20 +433,40 @@ def tile_diffscm_pb_kernel(
             old_share(0)
             old_share(1)
             old_share(2)
-            turn_xt(2)
+            flip_xt(8)
+            copy_xt(8)
+            vector_empties(8, 9)
+            flip_xt(9)
+            copy_xt(9)
+            vector_empties(9, 10)
+            flip_xt(10)
+            copy_xt(10)
+            vector_empties(10, 11)
+            flip_xt(11)
+            copy_xt(11)
+            vector_empties(11, 12)
             for n in range(2, 5):
                 function(n)
             flip_eps(0)
             noise(0)
             mean_product(0, 0)
             quantise(2)
-            vector_empties(8, 12)
-            turn_xt(3)
+            flip_xt(12)
+            copy_xt(12)
+            vector_empties(12, 13)
+            flip_xt(13)
+            copy_xt(13)
+            vector_empties(13, 14)
+            flip_xt(14)
+            copy_xt(14)
+            vector_empties(14, 15)
+            flip_xt(15)
+            copy_xt(15)
+            vector_empties(15, 16)
             flip_eps(1)
             for n in range(5, 8):
                 function(n)
             quantise(3)
-            vector_empties(12, 16)
             products(19)
             for n in range(8, max(len(items), 2 * ALL_PAIRS + 8)):
                 if n < len(items):
@@ -460,8 +487,7 @@ def tile_diffscm_pb_kernel(
                     if half == 0 and q % PAIRS == 0 and q // PAIRS + 2 < BATCHES:
                         eps_of[q // PAIRS + 2] = load_batch(eps_rows, q // PAIRS + 2, "eps_sb")
                     step_half(q, half)
+            while state["flips"] < 2 * ROW_TILES:
+                flip_next(2 * ROW_TILES)
             while state["blends"] < 2 * ROW_TILES:
-                flip_next(2 * ROW_TILES)
-                flip_next(2 * ROW_TILES)
-                blend_next()
                 blend_next()

@@ -275,6 +275,14 @@ def tile_diffscm_pb_kernel(
         def old_share(m):
             blend = blends.tile([P, FEATURES], F32)
             blend_of[m] = blend
+            if m >= 12:
+                nc.scalar.activation(
+                    out=blend[:],
+                    in_=x_of[m // BATCH][:, m % BATCH, :],
+                    func=ACT.Copy,
+                    scale=t_old[:, m : m + 1],
+                )
+                return
             nc.gpsimd.tensor_scalar(
                 out=blend[:],
                 in0=x_of[m // BATCH][:, m % BATCH, :],
@@ -356,7 +364,7 @@ def tile_diffscm_pb_kernel(
         def blend_next():
             n = state["blends"]
             if n < state["flips"]:
-                blend(n, n >= 22 and n % 2 == 0 and n < 30)
+                blend(n, 20 <= n < 28 and n % 2 == 0)
                 state["blends"] += 1
 
         def flip_next(limit):
@@ -478,7 +486,7 @@ def tile_diffscm_pb_kernel(
                         products(ahead[-1] + 1 + 2)
                     function(n)
                 for m in range(ROW_TILES):
-                    if n == (9 if m == 3 else 2 * m + (4 if m < 8 else 6)):
+                    if n == (9 if m == 3 else (m + 20 if m >= 12 else 2 * m + (4 if m < 8 else 6))):
                         if m % BATCH == 0 and m // BATCH >= 2:
                             x_of[m // BATCH] = load_batch(x_rows, m // BATCH, "x_sb")
                         old_share(m)

@@ -480,7 +480,7 @@ def tile_diffscm_pb_kernel(
                 if n < len(items):
                     for j in before[n]:
                         products(j + 1)
-                        evacuate(j, j % 4 == 0)
+                        evacuate(j, j % 2 == 0)
                     ahead = (before[n] or before[min(n + 1, len(items) - 1)])
                     if ahead:
                         products(ahead[-1] + 1 + 2)

@@ -364,7 +364,7 @@ def tile_diffscm_pb_kernel(
         def blend_next():
             n = state["blends"]
             if n < state["flips"]:
-                blend(n, 20 <= n < 28 and n % 2 == 0)
+                blend(n, 18 <= n < 26 and n % 2 == 0)
                 state["blends"] += 1
 
         def flip_next(limit):
@@ -480,7 +480,7 @@ def tile_diffscm_pb_kernel(
                 if n < len(items):
                     for j in before[n]:
                         products(j + 1)
-                        evacuate(j, j % 2 == 0)
+                        evacuate(j, j % 8 in (0, 2, 4))
                     ahead = (before[n] or before[min(n + 1, len(items) - 1)])
                     if ahead:
                         products(ahead[-1] + 1 + 2)

@@ -32,7 +32,7 @@ LN_FLOOR = 2.0**-60
 
 FLOPS = 2 * ROWS * FEATURES * 2 * FEATURES
 
-GROUPS = (1, 3, 4, 4, 3, 1)
+GROUPS = (4, 4, 4, 4)
 
 
 def tile_diffscm_pb_kernel(
@@ -102,8 +102,8 @@ def tile_diffscm_pb_kernel(
         load_weights(MEAN, Wm_words, Wm_scales)
         eps_of[0] = load_batch(eps_rows, 0, "eps_sb")
         load_xt_batch(2)
-        load_xt_batch(3)
         x_of[0] = load_batch(x_rows, 0, "x_sb")
+        load_xt_batch(3)
         eps_of[1] = load_batch(eps_rows, 1, "eps_sb")
         x_of[1] = load_batch(x_rows, 1, "x_sb")
 
@@ -345,7 +345,7 @@ def tile_diffscm_pb_kernel(
             items += [(1, q) for q in range(first, first + size)]
             first += size
         before = []
-        emptied = 16
+        emptied = 14
         for n in range(len(items)):
             kind, q = items[n]
             need = 2 * (q + 1) if kind == 0 else 0
@@ -436,11 +436,9 @@ def tile_diffscm_pb_kernel(
             evacuate(1)
             quantise(1)
             function(0)
-            function(1)
             vector_empties(2, 8)
-            old_share(0)
-            old_share(1)
-            old_share(2)
+            for n in range(1, 4):
+                function(n)
             flip_xt(8)
             copy_xt(8)
             vector_empties(8, 9)
@@ -453,29 +451,28 @@ def tile_diffscm_pb_kernel(
             flip_xt(11)
             copy_xt(11)
             vector_empties(11, 12)
-            for n in range(2, 5):
+            old_share(0)
+            old_share(1)
+            for n in range(4, 8):
                 function(n)
-            flip_eps(0)
-            noise(0)
-            mean_product(0, 0)
             quantise(2)
             flip_xt(12)
             copy_xt(12)
             vector_empties(12, 13)
             flip_xt(13)
             copy_xt(13)
-            vector_empties(13, 14)
             flip_xt(14)
             copy_xt(14)
-            vector_empties(14, 15)
+            vector_empties(13, 14)
             flip_xt(15)
             copy_xt(15)
-            vector_empties(15, 16)
+            flip_eps(0)
+            noise(0)
+            mean_product(0, 0)
+            old_share(2)
             flip_eps(1)
-            for n in range(5, 8):
-                function(n)
             quantise(3)
-            products(19)
+            products(17)
             for n in range(8, max(len(items), 2 * ALL_PAIRS + 8)):
                 if n < len(items):
                     for j in before[n]:
@@ -486,7 +483,7 @@ def tile_diffscm_pb_kernel(
                         products(ahead[-1] + 1 + 2)
                     function(n)
                 for m in range(ROW_TILES):
-                    if n == (9 if m == 3 else (m + 20 if m >= 12 else 2 * m + (4 if m < 8 else 6))):
+                    if n == (9 if m == 3 else (m + 20 if m >= 12 else 2 * m + (4 if m < 8 else 4))):
                         if m % BATCH == 0 and m // BATCH >= 2:
                             x_of[m // BATCH] = load_batch(x_rows, m // BATCH, "x_sb")
                         old_share(m)

@@ -46,8 +46,9 @@ def tile_diffscm_pb_kernel(
 
     with ExitStack() as ctx:
         const = ctx.enter_context(tc.tile_pool(name="const", bufs=1))
-        xt_tiles = ctx.enter_context(tc.tile_pool(name="xt_tiles", bufs=ROW_TILES))
+        xt_tiles = ctx.enter_context(tc.tile_pool(name="xt_tiles", bufs=12))
         loads = ctx.enter_context(tc.tile_pool(name="loads", bufs=2))
+        x_tiles = ctx.enter_context(tc.tile_pool(name="x_tiles", bufs=3))
         regroup = ctx.enter_context(tc.tile_pool(name="regroup", bufs=2))
         packed = ctx.enter_context(tc.tile_pool(name="packed", bufs=BATCHES))
         samples = ctx.enter_context(tc.tile_pool(name="samples", bufs=12))
@@ -60,7 +61,8 @@ def tile_diffscm_pb_kernel(
         mean_banks = ctx.enter_context(tc.psum_pool(name="mean_banks", bufs=2))
 
         def load_batch(source, b, label):
-            rows = loads.tile([P, BATCH, FEATURES], BF16, name=label, tag=label)
+            pool = x_tiles if label == "x_sb" else loads
+            rows = pool.tile([P, BATCH, FEATURES], BF16, name=label, tag=label)
             nc.sync.dma_start(out=rows[:], in_=source[:, b * BATCH : (b + 1) * BATCH, :])
             return rows
 
@@ -106,6 +108,7 @@ def tile_diffscm_pb_kernel(
         load_xt_batch(3)
         eps_of[1] = load_batch(eps_rows, 1, "eps_sb")
         x_of[1] = load_batch(x_rows, 1, "x_sb")
+        x_of[2] = load_batch(x_rows, 2, "x_sb")
 
         bias_square_bf = const.tile([P, P], BF16)
         nc.vector.memset(bias_square_bf[:], 0.0)
@@ -483,13 +486,13 @@ def tile_diffscm_pb_kernel(
                         products(ahead[-1] + 1 + 2)
                     function(n)
                 for m in range(ROW_TILES):
-                    if n == (9 if m == 3 else (m + 20 if m >= 12 else 2 * m + (4 if m < 8 else 4))):
-                        if m % BATCH == 0 and m // BATCH >= 2:
-                            x_of[m // BATCH] = load_batch(x_rows, m // BATCH, "x_sb")
+                    if n == (m + 20 if m >= 12 else 2 * m + 3 if m >= 3 else -1):
+                        if m == 4:
+                            x_of[3] = load_batch(x_rows, 3, "x_sb")
                         old_share(m)
                 q, half = (n - 8) // 2, (n - 8) % 2
                 if 0 <= q < ALL_PAIRS:
-                    if half == 0 and q % PAIRS == 0 and q // PAIRS + 2 < BATCHES:
+                    if half == 0 and q % PAIRS == 2 and q // PAIRS + 2 < BATCHES:
                         eps_of[q // PAIRS + 2] = load_batch(eps_rows, q // PAIRS + 2, "eps_sb")
                     step_half(q, half)
             while state["flips"] < 2 * ROW_TILES:

@@ -161,15 +161,11 @@ def tile_diffscm_pb_kernel(
         def quantise(b):
             codes = packed.tile([P, PASSES, BATCH, P], U32, align_bytes=64)
             code_scales = packed.tile([P, PASSES, BATCH, P], U8, align_bytes=64)
-            half = PASSES * BATCH * P // 2
-            flat_codes = codes[:].rearrange("p g i r -> p (g i r)")
-            flat_scales = code_scales[:].rearrange("p g i r -> p (g i r)")
-            for g in range(PASSES):
-                nc.vector.quantize_mx(
-                    out=flat_codes[:, g * half : (g + 1) * half].bitcast(FP8X4),
-                    scales=flat_scales[:, g * half : (g + 1) * half],
-                    in_=grouped_of[b][:, g * half * PACK : (g + 1) * half * PACK],
-                )
+            nc.vector.quantize_mx(
+                out=codes[:].rearrange("p g i r -> p (g i r)").bitcast(FP8X4),
+                scales=code_scales[:].rearrange("p g i r -> p (g i r)"),
+                in_=grouped_of[b][:],
+            )
             packed_of[b] = (codes, code_scales)
 
         def product(bank, head, b, c):
@@ -443,15 +439,15 @@ def tile_diffscm_pb_kernel(
             for n in range(1, 4):
                 function(n)
             flip_xt(8)
+            flip_xt(9)
             copy_xt(8)
             vector_empties(8, 9)
-            flip_xt(9)
             copy_xt(9)
             vector_empties(9, 10)
             flip_xt(10)
+            flip_xt(11)
             copy_xt(10)
             vector_empties(10, 11)
-            flip_xt(11)
             copy_xt(11)
             vector_empties(11, 12)
             old_share(0)
@@ -460,14 +456,14 @@ def tile_diffscm_pb_kernel(
                 function(n)
             quantise(2)
             flip_xt(12)
+            flip_xt(13)
             copy_xt(12)
             vector_empties(12, 13)
-            flip_xt(13)
             copy_xt(13)
-            flip_xt(14)
-            copy_xt(14)
             vector_empties(13, 14)
+            flip_xt(14)
             flip_xt(15)
+            copy_xt(14)
             copy_xt(15)
             flip_eps(0)
             noise(0)

from contextlib import ExitStack

import concourse.mybir as mybir
from concourse.masks import make_identity

F32 = mybir.dt.float32
BF16 = mybir.dt.bfloat16
I32 = mybir.dt.int32
U32 = mybir.dt.uint32
U8 = mybir.dt.uint8
FP8X4 = mybir.dt.float8_e4m3fn_x4
FP4X4 = mybir.dt.float4_e2m1fn_x4
ALU = mybir.AluOpType
ACT = mybir.ActivationFunctionType

P = 128
ROWS = 2048
FEATURES = 1024
PACK = 4
K_PASS = P * PACK
PASSES = FEATURES // K_PASS
ROW_TILES = ROWS // P
BATCH = 4
BATCHES = ROW_TILES // BATCH
BANK = 512
FEATURE_TILES = FEATURES // P
PAIRS = FEATURE_TILES // 2
ALL_PAIRS = BATCHES * PAIRS
WORDS = K_PASS // 2
SPREAD, MEAN = 0, 1
LN_FLOOR = 2.0**-60

FLOPS = 2 * ROWS * FEATURES * 2 * FEATURES

GROUPS = (4, 4, 4, 4)


def tile_diffscm_pb_kernel(
    tc, xt, eps, x, t_rand, Wm_words, Wm_scales, bm, Wv_words, Wv_scales, bv, out
):
    nc = tc.nc
    xt_rows = xt.rearrange("(p i) d -> p i d", i=ROW_TILES)
    eps_rows = eps.rearrange("(p i) d -> p i d", i=ROW_TILES)
    x_rows = x.rearrange("(p i) d -> p i d", i=ROW_TILES)
    out_rows = out.rearrange("(p i) d -> p i d", i=ROW_TILES)

    with ExitStack() as ctx:
        const = ctx.enter_context(tc.tile_pool(name="const", bufs=1))
        xt_tiles = ctx.enter_context(tc.tile_pool(name="xt_tiles", bufs=12))
        loads = ctx.enter_context(tc.tile_pool(name="loads", bufs=2))
        x_tiles = ctx.enter_context(tc.tile_pool(name="x_tiles", bufs=3))
        regroup = ctx.enter_context(tc.tile_pool(name="regroup", bufs=2))
        packed = ctx.enter_context(tc.tile_pool(name="packed", bufs=BATCHES))
        samples = ctx.enter_context(tc.tile_pool(name="samples", bufs=12))
        gates = ctx.enter_context(tc.tile_pool(name="gates", bufs=8))
        blends = ctx.enter_context(tc.tile_pool(name="blends", bufs=8))
        weights = ctx.enter_context(tc.tile_pool(name="weights", bufs=3))
        flip_banks = ctx.enter_context(tc.psum_pool(name="flip_banks", bufs=2))
        eps_banks = ctx.enter_context(tc.psum_pool(name="eps_banks", bufs=1))
        spread_banks = ctx.enter_context(tc.psum_pool(name="spread_banks", bufs=3))
        mean_banks = ctx.enter_context(tc.psum_pool(name="mean_banks", bufs=2))

        def load_batch(source, b, label):
            pool = x_tiles if label == "x_sb" else loads
            rows = pool.tile([P, BATCH, FEATURES], BF16, name=label, tag=label)
            nc.sync.dma_start(out=rows[:], in_=source[:, b * BATCH : (b + 1) * BATCH, :])
            return rows

        xt_of = {}

        def load_xt_batch(b):
            for i in range(BATCH):
                xt_sb = xt_tiles.tile([P, FEATURES], BF16)
                nc.sync.dma_start(out=xt_sb[:], in_=xt_rows[:, b * BATCH + i, :])
                xt_of[b * BATCH + i] = xt_sb

        identity = const.tile([P, P], F32)
        make_identity(nc, identity[:])
        w_scales = const.tile([P, 2, PASSES, FEATURES], U8, align_bytes=64)
        nc.vector.memset(w_scales[:].rearrange("p h g n -> p (h g n)").bitcast(I32), 0)
        identity_bf = const.tile([P, P], BF16)
        make_identity(nc, identity_bf[:])

        w_words = const.tile([P, 2, PASSES, 2 * FEATURES], U8, align_bytes=64)

        def load_weights(head, words, scale_rows):
            for quadrant in range(4):
                nc.sync.dma_start(
                    out=w_scales[32 * quadrant : 32 * quadrant + 4, head].bitcast(I32),
                    in_=scale_rows.bitcast(I32)[:, 4 * quadrant : 4 * quadrant + 4, :].rearrange(
                        "g r w -> r g w"
                    ),
                )
            nc.sync.dma_start(
                out=w_words[:, head].bitcast(I32),
                in_=words.bitcast(I32).rearrange("g p w -> p g w"),
            )

        eps_of = {}
        x_of = {}
        load_xt_batch(0)
        load_xt_batch(1)
        load_weights(SPREAD, Wv_words, Wv_scales)
        load_weights(MEAN, Wm_words, Wm_scales)
        eps_of[0] = load_batch(eps_rows, 0, "eps_sb")
        load_xt_batch(2)
        x_of[0] = load_batch(x_rows, 0, "x_sb")
        load_xt_batch(3)
        eps_of[1] = load_batch(eps_rows, 1, "eps_sb")
        x_of[1] = load_batch(x_rows, 1, "x_sb")
        x_of[2] = load_batch(x_rows, 2, "x_sb")

        bias_square_bf = const.tile([P, P], BF16)
        nc.vector.memset(bias_square_bf[:], 0.0)
        warm = const.tile([P, 1], F32)
        nc.vector.memset(warm[:], 0.0)
        nc.scalar.dma_start(
            out=bias_square_bf[0:FEATURE_TILES, :], in_=bv.rearrange("(c n) -> c n", n=P)
        )
        nc.scalar.dma_start(
            out=bias_square_bf[FEATURE_TILES : 2 * FEATURE_TILES, :],
            in_=bm.rearrange("(c n) -> c n", n=P),
        )
        t_bf = const.tile([P, ROW_TILES], BF16)
        nc.scalar.dma_start(out=t_bf[:], in_=t_rand.rearrange("(p i) o -> p (i o)", i=ROW_TILES))
        nc.scalar.activation(out=warm[:], in_=warm[:], func=ACT.Sigmoid)

        grouped_of = {}
        xt_flipped_of = {}
        packed_of = {}

        def flip_xt(m):
            row_words = xt_of[m][:].bitcast(F32)
            if m % 4 >= 2:
                flipped = mean_banks.tile([P, PASSES, 2, P], F32, tag="mean")
            else:
                flipped = flip_banks.tile([P, PASSES, 2, P], F32, tag="flip")
            for g in range(PASSES):
                for u in range(2):
                    nc.tensor.transpose(
                        flipped[:, g, u, :],
                        row_words[:, WORDS * g + u : WORDS * (g + 1) : 2],
                        identity[:],
                    )
            xt_flipped_of[m] = flipped

        def copy_xt(m, on_scalar=False):
            b, i = m // BATCH, m % BATCH
            if i == 0:
                grouped = regroup.tile([P, PASSES * BATCH * P * PACK], BF16, align_bytes=64)
                grouped_of[b] = grouped
            words = grouped_of[b][:].bitcast(F32).rearrange(
                "p (g i r u) -> p g i r u", g=PASSES, i=BATCH, u=2
            )
            source = xt_flipped_of[m][:].rearrange("p g u r -> p g r u")
            if on_scalar:
                nc.scalar.copy(out=words[:, :, i], in_=source)
            else:
                nc.vector.tensor_copy(out=words[:, :, i], in_=source)

        def quantise(b):
            codes = packed.tile([P, PASSES, BATCH, P], U32, align_bytes=64)
            code_scales = packed.tile([P, PASSES, BATCH, P], U8, align_bytes=64)
            nc.vector.quantize_mx(
                out=codes[:].rearrange("p g i r -> p (g i r)").bitcast(FP8X4),
                scales=code_scales[:].rearrange("p g i r -> p (g i r)"),
                in_=grouped_of[b][:],
            )
            packed_of[b] = (codes, code_scales)

        def product(bank, head, b, c):
            codes, code_scales = packed_of[b]
            for g in range(PASSES):
                nc.tensor.matmul_mx(
                    out=bank[:],
                    lhsT=w_words[:, head, g, 2 * c * P : 2 * (c + 1) * P].bitcast(FP4X4),
                    lhsT_scale=w_scales[:, head, g, c * P : (c + 1) * P],
                    rhs=codes[:, g].rearrange("p i r -> p (i r)").bitcast(FP8X4),
                    rhs_scale=code_scales[:, g].rearrange("p i r -> p (i r)"),
                    start=(g == 0),
                    stop=(g == PASSES - 1),
                )

        sample_of = {}
        gate_of = {}
        spread_of = {}
        mean_of = {}
        eps_flipped_of = {}
        sample_flipped_of = {}
        blend_of = {}

        def flat(tile_):
            return tile_[:].rearrange("p s b -> p (s b)")

        def spread_product(j):
            sums = spread_banks.tile([P, BANK], F32, tag="spread")
            product(sums, SPREAD, j // FEATURE_TILES, j % FEATURE_TILES)
            spread_of[j] = sums

        def evacuate(j, by_vector=False):
            q, side, c = j // 2, j % 2, j % FEATURE_TILES
            if side == 0:
                sample = samples.tile([P, 2, BANK], F32)
                sample_of[q] = sample
            if by_vector:
                nc.vector.tensor_scalar_add(
                    out=sample_of[q][:, side, :], in0=spread_of[j][:], scalar1=bias_col[:, c : c + 1]
                )
            else:
                nc.scalar.activation(
                    out=sample_of[q][:, side, :],
                    in_=spread_of[j][:],
                    func=ACT.Identity,
                    bias=bias_col[:, c : c + 1],
                )

        def sigmoid(q):
            gate = gates.tile([P, 2, BANK], F32)
            gate_of[q] = gate
            nc.scalar.activation(out=flat(gate), in_=flat(sample_of[q]), func=ACT.Sigmoid)

        def logarithm(q):
            nc.scalar.activation(
                out=flat(gate_of[q]), in_=flat(gate_of[q]), func=ACT.Ln, bias=LN_FLOOR
            )

        def subtract(q, on_vector=False):
            engine = nc.vector if on_vector else nc.gpsimd
            engine.tensor_tensor(
                out=flat(sample_of[q]), in0=flat(sample_of[q]), in1=flat(gate_of[q]), op=ALU.subtract
            )

        def flip_eps(q):
            b, pair = q // PAIRS, q % PAIRS
            eps_flipped = eps_banks.tile([P, 2, BATCH, P], BF16, tag="eps")
            for side in range(2):
                c = 2 * pair + side
                for i in range(BATCH):
                    nc.tensor.matmul(
                        eps_flipped[:, side, i, :],
                        lhsT=eps_of[b][:, i, c * P : (c + 1) * P],
                        rhs=identity_bf[:],
                        start=True,
                        stop=True,
                    )
            eps_flipped_of[q] = eps_flipped

        def noise(q):
            nc.vector.scalar_tensor_tensor(
                out=flat(sample_of[q]),
                in0=flat(sample_of[q]),
                scalar=0.0,
                in1=eps_flipped_of[q][:].rearrange("p s i r -> p (s i r)"),
                op0=ALU.max,
                op1=ALU.mult,
            )

        def mean_product(q, side):
            sums = mean_banks.tile([P, BANK], F32, tag="mean")
            product(sums, MEAN, q // PAIRS, 2 * (q % PAIRS) + side)
            mean_of[(q, side)] = sums

        def add_mean(q, side):
            c = FEATURE_TILES + 2 * (q % PAIRS) + side
            nc.vector.scalar_tensor_tensor(
                out=sample_of[q][:, side, :],
                in0=mean_of[(q, side)][:],
                scalar=bias_col[:, c : c + 1],
                in1=sample_of[q][:, side, :],
                op0=ALU.add,
                op1=ALU.add,
            )

        def old_share(m):
            blend = blends.tile([P, FEATURES], F32)
            blend_of[m] = blend
            if m >= 12:
                nc.scalar.activation(
                    out=blend[:],
                    in_=x_of[m // BATCH][:, m % BATCH, :],
                    func=ACT.Copy,
                    scale=t_old[:, m : m + 1],
                )
                return
            nc.gpsimd.tensor_scalar(
                out=blend[:],
                in0=x_of[m // BATCH][:, m % BATCH, :],
                scalar1=t_old[:, m : m + 1],
                scalar2=0.0,
                op0=ALU.mult,
                op1=ALU.add,
            )

        def split(n):
            return n // 8, (n % 8) // BATCH, n % BATCH

        def flip_sample(n):
            b, half, i = split(n)
            if n < 2 * ROW_TILES - BATCH:
                flipped = flip_banks.tile([P, BANK // P, P], F32, tag="flip")
            elif i < 3:
                flipped = spread_banks.tile([P, BANK // P, P], F32, tag="spread")
            else:
                flipped = mean_banks.tile([P, BANK // P, P], F32, tag="mean")
            for k in range(BANK // P):
                sample = sample_of[b * PAIRS + 2 * half + k // 2]
                nc.tensor.transpose(
                    flipped[:, k, :], sample[:, k % 2, i * P : (i + 1) * P], identity[:]
                )
            sample_flipped_of[n] = flipped

        def blend(n, split_blend=False):
            b, half, i = split(n)
            m = b * BATCH + i
            cols = slice(half * BANK, (half + 1) * BANK)
            if split_blend:
                weighed = weights.tile([P, BANK], F32)
                nc.scalar.activation(
                    out=weighed[:],
                    in_=sample_flipped_of[n][:].rearrange("p k n -> p (k n)"),
                    func=ACT.Copy,
                    scale=t_new[:, m : m + 1],
                )
                nc.gpsimd.tensor_tensor(
                    out=blend_of[m][:, cols], in0=weighed[:], in1=blend_of[m][:, cols], op=ALU.add
                )
                nc.sync.dma_start(out=out_rows[:, m, cols], in_=blend_of[m][:, cols])
                return
            nc.vector.scalar_tensor_tensor(
                out=blend_of[m][:, cols],
                in0=sample_flipped_of[n][:].rearrange("p k n -> p (k n)"),
                scalar=t_new[:, m : m + 1],
                in1=blend_of[m][:, cols],
                op0=ALU.mult,
                op1=ALU.add,
            )
            nc.sync.dma_start(out=out_rows[:, m, cols], in_=blend_of[m][:, cols])


        items = []
        first = 0
        for size in GROUPS:
            items += [(0, q) for q in range(first, first + size)]
            items += [(1, q) for q in range(first, first + size)]
            first += size
        before = []
        emptied = 14
        for n in range(len(items)):
            kind, q = items[n]
            need = 2 * (q + 1) if kind == 0 else 0
            count = max(need - emptied, 1 if n >= 12 else 0)
            count = max(min(count, 2 * ALL_PAIRS - emptied), 0)
            before.append(list(range(emptied, emptied + count)))
            emptied += count

        state = {"flips": 0, "blends": 0, "product": 0}

        def products(count):
            while state["product"] < min(count, 2 * ALL_PAIRS):
                spread_product(state["product"])
                state["product"] += 1

        def blend_next():
            n = state["blends"]
            if n < state["flips"]:
                blend(n, 18 <= n < 26 and n % 2 == 0)
                state["blends"] += 1

        def flip_next(limit):
            if state["flips"] < limit:
                flip_sample(state["flips"])
                state["flips"] += 1

        def function(n):
            kind, q = items[n]
            if kind == 0:
                sigmoid(q)
            else:
                logarithm(q)
                subtract(q)

        def vector_empties(first, last):
            for j in range(first, last):
                products(j + 1)
                evacuate(j, True)

        def turn_xt(b, on_scalar=()):
            for i in range(BATCH):
                flip_xt(BATCH * b + i)
                copy_xt(BATCH * b + i, i in on_scalar)

        def step_half(q, half):
            if half == 0:
                mean_product(q, 1)
                for k in range(2):
                    flip_next(4 * (q // 2))
                if q + 1 < ALL_PAIRS:
                    noise(q + 1)
                add_mean(q, 0)
                if q + 1 < ALL_PAIRS:
                    blend_next()
            else:
                if q + 2 < ALL_PAIRS:
                    flip_eps(q + 2)
                if q + 1 < ALL_PAIRS:
                    mean_product(q + 1, 0)
                add_mean(q, 1)
                if q + 1 < ALL_PAIRS:
                    blend_next()

        t_new = const.tile([P, ROW_TILES], F32)
        t_old = const.tile([P, ROW_TILES], F32)
        bias_square = const.tile([P, P], F32)
        bias_col = const.tile([P, 2 * FEATURE_TILES], F32)
        every = {
            mybir.EngineType.PE,
            mybir.EngineType.Activation,
            mybir.EngineType.DVE,
            mybir.EngineType.Pool,
        }
        with tc.manual_schedule(engines=every):
            turn_xt(0, (1, 3))
            nc.vector.tensor_copy(out=bias_square[:], in_=bias_square_bf[:])
            bias_flipped = eps_banks.tile([P, P], F32, tag="eps")
            nc.tensor.transpose(bias_flipped[:], bias_square[:], identity[:])
            nc.vector.tensor_copy(out=bias_col[:], in_=bias_flipped[:, 0 : 2 * FEATURE_TILES])
            quantise(0)
            nc.vector.tensor_copy(out=t_new[:], in_=t_bf[:])
            nc.vector.tensor_scalar(
                out=t_old[:], in0=t_bf[:], scalar1=-1.0, scalar2=1.0, op0=ALU.mult, op1=ALU.add
            )
            turn_xt(1, (0, 1, 2, 3))
            products(2)
            evacuate(0)
            evacuate(1)
            quantise(1)
            function(0)
            vector_empties(2, 8)
            for n in range(1, 4):
                function(n)
            flip_xt(8)
            flip_xt(9)
            copy_xt(8)
            vector_empties(8, 9)
            copy_xt(9)
            vector_empties(9, 10)
            flip_xt(10)
            flip_xt(11)
            copy_xt(10)
            vector_empties(10, 11)
            copy_xt(11)
            vector_empties(11, 12)
            old_share(0)
            old_share(1)
            for n in range(4, 8):
                function(n)
            quantise(2)
            flip_xt(12)
            flip_xt(13)
            copy_xt(12)
            vector_empties(12, 13)
            copy_xt(13)
            vector_empties(13, 14)
            flip_xt(14)
            flip_xt(15)
            copy_xt(14)
            copy_xt(15)
            flip_eps(0)
            noise(0)
            mean_product(0, 0)
            old_share(2)
            flip_eps(1)
            quantise(3)
            products(17)
            for n in range(8, max(len(items), 2 * ALL_PAIRS + 8)):
                if n < len(items):
                    for j in before[n]:
                        products(j + 1)
                        evacuate(j, j % 8 in (0, 2, 4))
                    ahead = (before[n] or before[min(n + 1, len(items) - 1)])
                    if ahead:
                        products(ahead[-1] + 1 + 2)
                    function(n)
                for m in range(ROW_TILES):
                    if n == (m + 20 if m >= 12 else 2 * m + 3 if m >= 3 else -1):
                        if m == 4:
                            x_of[3] = load_batch(x_rows, 3, "x_sb")
                        old_share(m)
                q, half = (n - 8) // 2, (n - 8) % 2
                if 0 <= q < ALL_PAIRS:
                    if half == 0 and q % PAIRS == 2 and q // PAIRS + 2 < BATCHES:
                        eps_of[q // PAIRS + 2] = load_batch(eps_rows, q // PAIRS + 2, "eps_sb")
                    step_half(q, half)
            while state["flips"] < 2 * ROW_TILES:
                flip_next(2 * ROW_TILES)
            while state["blends"] < 2 * ROW_TILES:
                blend_next()
